import numpy as np
import ml_dtypes


def mxq(x, axis, fmt="e4m3"):
    dtype, down = {"e4m3": (ml_dtypes.float8_e4m3fn, 7), "e5m2": (ml_dtypes.float8_e5m2, 14)}[fmt]
    v = np.moveaxis(np.asarray(x, np.float32).astype(ml_dtypes.bfloat16).astype(np.float64), axis, -1)
    blocks = v.reshape(v.shape[:-1] + (-1, 32))
    amax = np.abs(blocks).max(-1, keepdims=True)
    byte = np.maximum(np.where(amax > 0, np.frexp(amax)[1] - 1 + 127, 0) - down, 1)
    scale = np.exp2(byte - 127.0)
    codes = (blocks / scale).astype(np.float32).astype(dtype).astype(np.float64)
    return np.moveaxis((codes * scale).reshape(v.shape), -1, axis)


WIDE = False


def mx_kscale(k):
    if not WIDE:
        return np.ones(k)
    levels = np.array([10, -10, 5, -5, 0])
    a = np.random.permutation(np.resize(levels, k // 512 * 4)).reshape(k // 512, 4)
    idx = np.arange(k)
    return np.exp2(a[idx // 512, idx % 128 // 32])


BF16 = ml_dtypes.bfloat16


def bf(x):
    return np.asarray(x, np.float32).astype(BF16)


def f64(x):
    return np.asarray(x).astype(np.float64)


E2M1 = np.array([0.0, 0.5, 1.0, 1.5, 2.0, 3.0, 4.0, 6.0, -0.0, -0.5, -1.0, -1.5, -2.0, -3.0, -4.0, -6.0])


def pack_weight(w, fmt):
    k, n = w.shape
    w = f64(bf(w)).reshape(k // 32, 32, n)
    amax = np.abs(w).max(1)
    if fmt == "e4m3":
        byte = np.frexp(amax)[1] - 1 + 127 - 7
    else:
        mant, ex = np.frexp(amax / 6.0)
        byte = np.where(mant > 0.5, ex, ex - 1) + 127
    byte = np.clip(np.where(amax > 0, byte, 1), 1, 254)
    scaled = (w * np.exp2(127.0 - byte)[:, None, :]).reshape(k, n).astype(np.float32)
    by_word = np.ascontiguousarray(scaled.reshape(k // 512, 128, 4, n).transpose(0, 1, 3, 2))
    if fmt == "e4m3":
        words = by_word.astype(ml_dtypes.float8_e4m3fn).view(np.uint8)
    else:
        c = by_word.astype(ml_dtypes.float4_e2m1fn).view(np.uint8) & 0xF
        words = c[..., 0::2] | (c[..., 1::2] << 4)
    return np.ascontiguousarray(words), np.ascontiguousarray(byte.astype(np.uint8).reshape(k // 512, 16, n))


def unpack_weight(words, scales, fmt):
    g, p, n, _ = words.shape
    if fmt == "e4m3":
        vals = np.ascontiguousarray(words).view(ml_dtypes.float8_e4m3fn).astype(np.float64)
    else:
        nib = np.empty((g, p, n, 4), np.uint8)
        nib[..., 0::2] = words & 0xF
        nib[..., 1::2] = words >> 4
        vals = E2M1[nib]
    vals = vals * np.repeat(np.exp2(scales.astype(np.float64) - 127.0), 8, axis=1)[..., None]
    return vals.transpose(0, 1, 3, 2).reshape(g * 512, n)


B, I, H = 512, 1024, 1024
FMT = "e4m3"


def sigmoid(v):
    return 1.0 / (1.0 + np.exp(-v))


def setup_inputs():
    s = mx_kscale(I + H)
    sx, sh = s[:I], s[I:]

    def wx():
        return pack_weight((np.random.standard_normal((H, I)) * 0.7 / np.sqrt(I) / sx).T, FMT)

    def wh():
        return pack_weight((np.random.standard_normal((H, H)) * 0.7 / np.sqrt(H) / sh).T, FMT)

    def bias():
        return bf(np.random.standard_normal(H) * 0.3)

    out = {}
    out["x"] = bf(np.random.standard_normal((B, I)) * sx)
    out["h"] = bf(np.random.standard_normal((B, H)) * sh)
    out["c"] = bf(np.random.standard_normal((B, H)))
    for name in ("weight_ii", "weight_if", "weight_ig", "weight_io"):
        words, scales = wx()
        out[name + "_words"] = words
        out[name + "_scales"] = scales
    for name in ("weight_hi", "weight_hf", "weight_hg", "weight_ho"):
        words, scales = wh()
        out[name + "_words"] = words
        out[name + "_scales"] = scales
    for name in ("bias_i", "bias_f", "bias_g", "bias_o"):
        out[name] = bias()
    return out


def reference(x, h, c,
              weight_ii_words, weight_ii_scales, weight_if_words, weight_if_scales,
              weight_ig_words, weight_ig_scales, weight_io_words, weight_io_scales,
              weight_hi_words, weight_hi_scales, weight_hf_words, weight_hf_scales,
              weight_hg_words, weight_hg_scales, weight_ho_words, weight_ho_scales,
              bias_i, bias_f, bias_g, bias_o):
    W_x = np.concatenate([unpack_weight(weight_ii_words, weight_ii_scales, FMT).T,
                          unpack_weight(weight_if_words, weight_if_scales, FMT).T,
                          unpack_weight(weight_ig_words, weight_ig_scales, FMT).T,
                          unpack_weight(weight_io_words, weight_io_scales, FMT).T], axis=0)
    W_h = np.concatenate([unpack_weight(weight_hi_words, weight_hi_scales, FMT).T,
                          unpack_weight(weight_hf_words, weight_hf_scales, FMT).T,
                          unpack_weight(weight_hg_words, weight_hg_scales, FMT).T,
                          unpack_weight(weight_ho_words, weight_ho_scales, FMT).T], axis=0)
    b = np.concatenate([f64(bias_i), f64(bias_f), f64(bias_g), f64(bias_o)], axis=0)
    z = np.concatenate([f64(x), f64(h)], axis=1)
    W = np.concatenate([W_x, W_h], axis=1)
    gates = (mxq(z, 1, "e4m3") @ W.T) + b
    gi, gf, gg, go = np.split(gates, 4, axis=1)
    i = sigmoid(gi)
    f = sigmoid(gf)
    g = np.tanh(gg)
    o = sigmoid(go)
    c_new = f * c_in(c) + i * g
    h_new = o * np.tanh(c_new)
    return (h_new, c_new)


def c_in(c):
    return f64(c)

@@ -1,0 +1,236 @@
+from contextlib import ExitStack
+
+import concourse.mybir as mybir
+from concourse.masks import make_identity
+
+F32 = mybir.dt.float32
+BF16 = mybir.dt.bfloat16
+I32 = mybir.dt.int32
+U32 = mybir.dt.uint32
+U8 = mybir.dt.uint8
+FP8X4 = mybir.dt.float8_e4m3fn_x4
+SIGMOID = mybir.ActivationFunctionType.Sigmoid
+TANH = mybir.ActivationFunctionType.Tanh
+ADD = mybir.AluOpType.add
+MULT = mybir.AluOpType.mult
+
+P = 128
+PACK = 4
+K_PASS = P * PACK
+BATCH, FEATURES, HIDDEN = 512, 1024, 1024
+SOURCES = 2
+GROUPS = FEATURES // K_PASS
+PASSES = SOURCES * GROUPS
+M_TILES = BATCH // P
+M_PAIRS = M_TILES // 2
+N_TILE = 512
+N_HALVES = HIDDEN // N_TILE
+GATES = 4
+PLANE_ROWS = 4
+
+FLOPS = 2 * BATCH * (SOURCES * FEATURES) * (GATES * HIDDEN)
+
+
+def tile_forcedgpulstmcell_kernel(
+    tc,
+    x, h, c,
+    weight_ii_words, weight_ii_scales, weight_if_words, weight_if_scales,
+    weight_ig_words, weight_ig_scales, weight_io_words, weight_io_scales,
+    weight_hi_words, weight_hi_scales, weight_hf_words, weight_hf_scales,
+    weight_hg_words, weight_hg_scales, weight_ho_words, weight_ho_scales,
+    bias_i, bias_f, bias_g, bias_o,
+    out_0, out_1,
+):
+    nc = tc.nc
+    gate_inputs = (
+        ((weight_ii_words, weight_hi_words), (weight_ii_scales, weight_hi_scales), bias_i),
+        ((weight_ig_words, weight_hg_words), (weight_ig_scales, weight_hg_scales), bias_g),
+        ((weight_if_words, weight_hf_words), (weight_if_scales, weight_hf_scales), bias_f),
+        ((weight_io_words, weight_ho_words), (weight_io_scales, weight_ho_scales), bias_o),
+    )
+    GATE_I, GATE_G, GATE_F, GATE_O = 0, 1, 2, 3
+
+    with ExitStack() as ctx:
+        const = ctx.enter_context(tc.tile_pool(name="const", bufs=1))
+        acts = ctx.enter_context(tc.tile_pool(name="acts", bufs=1))
+        weights = ctx.enter_context(tc.tile_pool(name="weights", bufs=1))
+        work = ctx.enter_context(tc.tile_pool(name="work", bufs=M_TILES))
+        psum = ctx.enter_context(tc.psum_pool(name="psum", bufs=8))
+
+        warm = const.tile([P, 1], F32)
+        nc.vector.memset(warm[:], 0.0)
+        nc.scalar.activation(out=warm[:], in_=warm[:], func=SIGMOID)
+
+        ident_bf16 = const.tile([P, P], BF16)
+        make_identity(nc, ident_bf16[:])
+        ident_f32 = const.tile([P, P], F32)
+        make_identity(nc, ident_f32[:])
+
+        bias_rows = const.tile([P, N_TILE], BF16)
+        nc.vector.memset(bias_rows[:], 0.0)
+        for q in range(GATES):
+            nc.scalar.dma_start(
+                out=bias_rows[N_HALVES * q : N_HALVES * (q + 1), :],
+                in_=gate_inputs[q][2].rearrange("(j n) -> j n", j=N_HALVES),
+            )
+
+        raw = {}
+        for s, source in enumerate((x, h)):
+            by_pair = source.rearrange("(mp m p) k -> mp p m k", m=2, p=P)
+            for mp in range(M_PAIRS):
+                raw[s, mp] = acts.tile([P, 2, FEATURES], BF16, name="raw_%d_%d" % (s, mp))
+                nc.scalar.dma_start(out=raw[s, mp][:], in_=by_pair[mp])
+
+        w_planes = []
+        for q in range(GATES):
+            planes = weights.tile([P, HIDDEN], U8, name="w_planes_%d" % q, align_bytes=64)
+            nc.vector.memset(planes[:].bitcast(I32), 0)
+            w_planes.append(planes)
+
+        def load_scales(q):
+            for s in range(SOURCES):
+                for quadrant in range(4):
+                    first = 32 * quadrant + GROUPS * PLANE_ROWS * s
+                    nc.sync.dma_start(
+                        out=w_planes[q][first : first + GROUPS * PLANE_ROWS, :].bitcast(I32),
+                        in_=gate_inputs[q][1][s][
+                            :, PLANE_ROWS * quadrant : PLANE_ROWS * (quadrant + 1), :
+                        ].bitcast(I32),
+                    )
+
+        w_words = {}
+
+        def load_words(q, j):
+            for s in range(SOURCES):
+                for g in range(GROUPS):
+                    k = GROUPS * s + g
+                    w_words[q, k, j] = weights.tile(
+                        [P, N_TILE], U32, name="w_words_%d_%d_%d" % (q, k, j), align_bytes=64
+                    )
+                    by_bytes = gate_inputs[q][0][s][g].rearrange("p n t -> p (n t)")
+                    nc.sync.dma_start(
+                        out=w_words[q, k, j][:].bitcast(I32),
+                        in_=by_bytes[:, PACK * N_TILE * j : PACK * N_TILE * (j + 1)].bitcast(I32),
+                    )
+
+        c_half = []
+        c_by_tile = c.rearrange("(m p) n -> p m n", p=P)
+
+        def load_c(j):
+            c_half.append(acts.tile([P, M_TILES, N_TILE], BF16, name="c_half_%d" % j))
+            nc.sync.dma_start(out=c_half[j][:], in_=c_by_tile[:, :, N_TILE * j : N_TILE * (j + 1)])
+
+        for j in range(N_HALVES):
+            for q in range(GATES):
+                if j == 0:
+                    load_scales(q)
+                if q == GATE_F:
+                    load_c(j)
+                load_words(q, j)
+
+        bias_all = const.tile([P, GATES * N_HALVES, N_TILE], F32)
+        for r in range(GATES * N_HALVES):
+            spread = psum.tile([P, N_TILE], F32, tag="bank")
+            nc.tensor.matmul(
+                out=spread[:],
+                lhsT=ident_bf16[:, r : r + 1].to_broadcast([P, P]),
+                rhs=bias_rows[:],
+                start=True,
+                stop=True,
+            )
+            if r % 2 == 0:
+                nc.vector.tensor_copy(out=bias_all[:, r, :], in_=spread[:])
+            else:
+                nc.scalar.copy(out=bias_all[:, r, :], in_=spread[:])
+
+        z_codes = {}
+        z_scales = {}
+        for s in range(SOURCES):
+            for mp in range(M_PAIRS):
+                words = raw[s, mp][:].bitcast(F32)
+                for g in range(GROUPS):
+                    k = GROUPS * s + g
+                    flipped = psum.tile([P, 2, 2 * P], F32, tag="bank")
+                    for u in range(2):
+                        for m in range(2):
+                            nc.tensor.transpose(
+                                flipped[:, u, P * m : P * (m + 1)],
+                                words[:, m, 2 * P * g + u : 2 * P * (g + 1) : 2],
+                                ident_f32[:],
+                            )
+                    grouped = acts.tile(
+                        [P, 2 * P, PACK], BF16, name="grouped_%d_%d" % (k, mp), align_bytes=64
+                    )
+                    grouped_flat = grouped[:].rearrange("p b t -> p (b t)")
+                    grouped_words = grouped_flat.bitcast(F32).rearrange("p (b u) -> p b u", u=2)
+                    if g % 2 == 0:
+                        nc.vector.tensor_copy(
+                            out=grouped_words, in_=flipped[:].rearrange("p u b -> p b u")
+                        )
+                    else:
+                        nc.scalar.copy(out=grouped_words, in_=flipped[:].rearrange("p u b -> p b u"))
+                    z_codes[k, mp] = acts.tile(
+                        [P, 2 * P], U32, name="z_codes_%d_%d" % (k, mp), align_bytes=64
+                    )
+                    z_scales[k, mp] = acts.tile(
+                        [P, 2 * P], U8, name="z_scales_%d_%d" % (k, mp), align_bytes=64
+                    )
+                    nc.vector.quantize_mx(
+                        out=z_codes[k, mp][:].bitcast(FP8X4),
+                        scales=z_scales[k, mp][:],
+                        in_=grouped_flat,
+                    )
+
+        def gate_values(q, j, func):
+            sums = [
+                psum.tile([P, N_TILE], F32, tag="bank", name="sums_%d" % m) for m in range(M_TILES)
+            ]
+            for k in range(PASSES):
+                for m in range(M_TILES):
+                    rows = slice(P * (m % 2), P * (m % 2 + 1))
+                    nc.tensor.matmul_mx(
+                        out=sums[m][:],
+                        lhsT=z_codes[k, m // 2][:, rows].bitcast(FP8X4),
+                        lhsT_scale=z_scales[k, m // 2][:, rows],
+                        rhs=w_words[q, k, j][:].bitcast(FP8X4),
+                        rhs_scale=w_planes[q][PLANE_ROWS * k : P, N_TILE * j : N_TILE * (j + 1)],
+                        start=(k == 0),
+                        stop=(k == PASSES - 1),
+                    )
+            values = []
+            for m in range(M_TILES):
+                value = work.tile([P, N_TILE], F32, tag="gate_%d" % q, name="gate_%d" % q)
+                nc.vector.tensor_tensor(
+                    out=value[:], in0=sums[m][:], in1=bias_all[:, N_HALVES * q + j, :], op=ADD
+                )
+                nc.scalar.activation(out=value[:], in_=value[:], func=func)
+                values.append(value)
+            return values
+
+        for j in range(N_HALVES):
+            columns = slice(N_TILE * j, N_TILE * (j + 1))
+            gate_i = gate_values(GATE_I, j, SIGMOID)
+            gate_g = gate_values(GATE_G, j, TANH)
+            new_part = []
+            for m in range(M_TILES):
+                new_part.append(work.tile([P, N_TILE], F32, tag="new_part", name="new_part"))
+                nc.gpsimd.tensor_tensor(
+                    out=new_part[m][:], in0=gate_i[m][:], in1=gate_g[m][:], op=MULT
+                )
+            gate_f = gate_values(GATE_F, j, SIGMOID)
+            tanh_c = []
+            for m in range(M_TILES):
+                kept_part = work.tile([P, N_TILE], F32, tag="kept_part")
+                nc.gpsimd.tensor_tensor(
+                    out=kept_part[:], in0=gate_f[m][:], in1=c_half[j][:, m, :], op=MULT
+                )
+                c_new = work.tile([P, N_TILE], F32, tag="c_new")
+                nc.vector.tensor_tensor(out=c_new[:], in0=kept_part[:], in1=new_part[m][:], op=ADD)
+                nc.sync.dma_start(out=out_1[P * m : P * (m + 1), columns], in_=c_new[:])
+                tanh_c.append(work.tile([P, N_TILE], F32, tag="tanh_c", name="tanh_c"))
+                nc.scalar.activation(out=tanh_c[m][:], in_=c_new[:], func=TANH)
+            gate_o = gate_values(GATE_O, j, SIGMOID)
+            for m in range(M_TILES):
+                h_new = work.tile([P, N_TILE], F32, tag="h_new")
+                nc.vector.tensor_tensor(out=h_new[:], in0=gate_o[m][:], in1=tanh_c[m][:], op=MULT)
+                nc.sync.dma_start(out=out_0[P * m : P * (m + 1), columns], in_=h_new[:])

@@ -57,14 +57,12 @@ def tile_forcedgpulstmcell_kernel(
         work = ctx.enter_context(tc.tile_pool(name="work", bufs=M_TILES))
         psum = ctx.enter_context(tc.psum_pool(name="psum", bufs=8))
 
-        warm = const.tile([P, 1], F32)
-        nc.vector.memset(warm[:], 0.0)
-        nc.scalar.activation(out=warm[:], in_=warm[:], func=SIGMOID)
-
-        ident_bf16 = const.tile([P, P], BF16)
-        make_identity(nc, ident_bf16[:])
-        ident_f32 = const.tile([P, P], F32)
-        make_identity(nc, ident_f32[:])
+        raw = {}
+        for s, source in enumerate((x, h)):
+            by_pair = source.rearrange("(mp m p) k -> mp p m k", m=2, p=P)
+            for mp in range(M_PAIRS):
+                raw[s, mp] = acts.tile([P, 2, FEATURES], BF16, name="raw_%d_%d" % (s, mp))
+                nc.sync.dma_start(out=raw[s, mp][:], in_=by_pair[mp])
 
         bias_rows = const.tile([P, N_TILE], BF16)
         nc.vector.memset(bias_rows[:], 0.0)
@@ -74,12 +72,14 @@ def tile_forcedgpulstmcell_kernel(
                 in_=gate_inputs[q][2].rearrange("(j n) -> j n", j=N_HALVES),
             )
 
-        raw = {}
-        for s, source in enumerate((x, h)):
-            by_pair = source.rearrange("(mp m p) k -> mp p m k", m=2, p=P)
-            for mp in range(M_PAIRS):
-                raw[s, mp] = acts.tile([P, 2, FEATURES], BF16, name="raw_%d_%d" % (s, mp))
-                nc.scalar.dma_start(out=raw[s, mp][:], in_=by_pair[mp])
+        warm = const.tile([P, 1], F32)
+        nc.vector.memset(warm[:], 0.0)
+        nc.scalar.activation(out=warm[:], in_=warm[:], func=SIGMOID)
+
+        ident_bf16 = const.tile([P, P], BF16)
+        make_identity(nc, ident_bf16[:])
+        ident_f32 = const.tile([P, P], F32)
+        make_identity(nc, ident_f32[:])
 
         w_planes = []
         for q in range(GATES):
@@ -128,20 +128,19 @@ def tile_forcedgpulstmcell_kernel(
                     load_c(j)
                 load_words(q, j)
 
-        bias_all = const.tile([P, GATES * N_HALVES, N_TILE], F32)
-        for r in range(GATES * N_HALVES):
-            spread = psum.tile([P, N_TILE], F32, tag="bank")
-            nc.tensor.matmul(
-                out=spread[:],
-                lhsT=ident_bf16[:, r : r + 1].to_broadcast([P, P]),
-                rhs=bias_rows[:],
-                start=True,
-                stop=True,
-            )
-            if r % 2 == 0:
-                nc.vector.tensor_copy(out=bias_all[:, r, :], in_=spread[:])
-            else:
-                nc.scalar.copy(out=bias_all[:, r, :], in_=spread[:])
+        bias_all = const.tile([P, GATES, N_HALVES, N_TILE], BF16)
+        for q in range(GATES):
+            spread = psum.tile([P, N_HALVES, N_TILE], BF16, tag="bank")
+            for j in range(N_HALVES):
+                r = N_HALVES * q + j
+                nc.tensor.matmul(
+                    out=spread[:, j, :],
+                    lhsT=ident_bf16[:, r : r + 1].to_broadcast([P, P]),
+                    rhs=bias_rows[:],
+                    start=True,
+                    stop=True,
+                )
+            nc.scalar.copy(out=bias_all[:, q, :, :], in_=spread[:])
 
         z_codes = {}
         z_scales = {}
@@ -181,27 +180,24 @@ def tile_forcedgpulstmcell_kernel(
                         in_=grouped_flat,
                     )
 
-        def gate_values(q, j, func):
-            sums = [
-                psum.tile([P, N_TILE], F32, tag="bank", name="sums_%d" % m) for m in range(M_TILES)
-            ]
+        def gate_values(q, j, mp, func):
+            values = []
+            sums = [psum.tile([P, N_TILE], F32, tag="bank", name="sums_%d" % m) for m in range(2)]
             for k in range(PASSES):
-                for m in range(M_TILES):
-                    rows = slice(P * (m % 2), P * (m % 2 + 1))
+                for m in range(2):
                     nc.tensor.matmul_mx(
                         out=sums[m][:],
-                        lhsT=z_codes[k, m // 2][:, rows].bitcast(FP8X4),
-                        lhsT_scale=z_scales[k, m // 2][:, rows],
+                        lhsT=z_codes[k, mp][:, P * m : P * (m + 1)].bitcast(FP8X4),
+                        lhsT_scale=z_scales[k, mp][:, P * m : P * (m + 1)],
                         rhs=w_words[q, k, j][:].bitcast(FP8X4),
                         rhs_scale=w_planes[q][PLANE_ROWS * k : P, N_TILE * j : N_TILE * (j + 1)],
                         start=(k == 0),
                         stop=(k == PASSES - 1),
                     )
-            values = []
-            for m in range(M_TILES):
+            for m in range(2):
                 value = work.tile([P, N_TILE], F32, tag="gate_%d" % q, name="gate_%d" % q)
                 nc.vector.tensor_tensor(
-                    out=value[:], in0=sums[m][:], in1=bias_all[:, N_HALVES * q + j, :], op=ADD
+                    out=value[:], in0=sums[m][:], in1=bias_all[:, q, j, :], op=ADD
                 )
                 nc.scalar.activation(out=value[:], in_=value[:], func=func)
                 values.append(value)
@@ -209,28 +205,39 @@ def tile_forcedgpulstmcell_kernel(
 
         for j in range(N_HALVES):
             columns = slice(N_TILE * j, N_TILE * (j + 1))
-            gate_i = gate_values(GATE_I, j, SIGMOID)
-            gate_g = gate_values(GATE_G, j, TANH)
+            gate_i = []
+            for mp in range(M_PAIRS):
+                gate_i.extend(gate_values(GATE_I, j, mp, SIGMOID))
             new_part = []
-            for m in range(M_TILES):
-                new_part.append(work.tile([P, N_TILE], F32, tag="new_part", name="new_part"))
-                nc.gpsimd.tensor_tensor(
-                    out=new_part[m][:], in0=gate_i[m][:], in1=gate_g[m][:], op=MULT
-                )
-            gate_f = gate_values(GATE_F, j, SIGMOID)
+            for mp in range(M_PAIRS):
+                gate_g = gate_values(GATE_G, j, mp, TANH)
+                for m in range(2):
+                    new_part.append(work.tile([P, N_TILE], F32, tag="new_part", name="new_part"))
+                    nc.gpsimd.tensor_tensor(
+                        out=new_part[2 * mp + m][:], in0=gate_i[2 * mp + m][:], in1=gate_g[m][:], op=MULT
+                    )
             tanh_c = []
-            for m in range(M_TILES):
-                kept_part = work.tile([P, N_TILE], F32, tag="kept_part")
-                nc.gpsimd.tensor_tensor(
-                    out=kept_part[:], in0=gate_f[m][:], in1=c_half[j][:, m, :], op=MULT
-                )
-                c_new = work.tile([P, N_TILE], F32, tag="c_new")
-                nc.vector.tensor_tensor(out=c_new[:], in0=kept_part[:], in1=new_part[m][:], op=ADD)
-                nc.sync.dma_start(out=out_1[P * m : P * (m + 1), columns], in_=c_new[:])
-                tanh_c.append(work.tile([P, N_TILE], F32, tag="tanh_c", name="tanh_c"))
-                nc.scalar.activation(out=tanh_c[m][:], in_=c_new[:], func=TANH)
-            gate_o = gate_values(GATE_O, j, SIGMOID)
-            for m in range(M_TILES):
-                h_new = work.tile([P, N_TILE], F32, tag="h_new")
-                nc.vector.tensor_tensor(out=h_new[:], in0=gate_o[m][:], in1=tanh_c[m][:], op=MULT)
-                nc.sync.dma_start(out=out_0[P * m : P * (m + 1), columns], in_=h_new[:])
+            for mp in range(M_PAIRS):
+                gate_f = gate_values(GATE_F, j, mp, SIGMOID)
+                for m in range(2):
+                    tile_rows = slice(P * (2 * mp + m), P * (2 * mp + m + 1))
+                    kept_part = work.tile([P, N_TILE], F32, tag="kept_part")
+                    nc.gpsimd.tensor_tensor(
+                        out=kept_part[:], in0=gate_f[m][:], in1=c_half[j][:, 2 * mp + m, :], op=MULT
+                    )
+                    c_new = work.tile([P, N_TILE], F32, tag="c_new")
+                    nc.vector.tensor_tensor(
+                        out=c_new[:], in0=kept_part[:], in1=new_part[2 * mp + m][:], op=ADD
+                    )
+                    nc.sync.dma_start(out=out_1[tile_rows, columns], in_=c_new[:])
+                    tanh_c.append(work.tile([P, N_TILE], F32, tag="tanh_c", name="tanh_c"))
+                    nc.scalar.activation(out=tanh_c[2 * mp + m][:], in_=c_new[:], func=TANH)
+            for mp in range(M_PAIRS):
+                gate_o = gate_values(GATE_O, j, mp, SIGMOID)
+                for m in range(2):
+                    tile_rows = slice(P * (2 * mp + m), P * (2 * mp + m + 1))
+                    h_new = work.tile([P, N_TILE], F32, tag="h_new")
+                    nc.vector.tensor_tensor(
+                        out=h_new[:], in0=gate_o[m][:], in1=tanh_c[2 * mp + m][:], op=MULT
+                    )
+                    nc.sync.dma_start(out=out_0[tile_rows, columns], in_=h_new[:])

@@ -26,6 +26,7 @@ M_PAIRS = M_TILES // 2
 N_TILE = 512
 N_HALVES = HIDDEN // N_TILE
 GATES = 4
+LAG = 2
 PLANE_ROWS = 4
 
 FLOPS = 2 * BATCH * (SOURCES * FEATURES) * (GATES * HIDDEN)
@@ -56,6 +57,15 @@ def tile_forcedgpulstmcell_kernel(
         weights = ctx.enter_context(tc.tile_pool(name="weights", bufs=1))
         work = ctx.enter_context(tc.tile_pool(name="work", bufs=M_TILES))
         psum = ctx.enter_context(tc.psum_pool(name="psum", bufs=8))
+        ctx.enter_context(tc.manual_schedule())
+
+        bias_rows = const.tile([P, N_TILE], BF16)
+        nc.vector.memset(bias_rows[:], 0.0)
+        for q in range(GATES):
+            nc.sync.dma_start(
+                out=bias_rows[N_HALVES * q : N_HALVES * (q + 1), :],
+                in_=gate_inputs[q][2].rearrange("(j n) -> j n", j=N_HALVES),
+            )
 
         raw = {}
         for s, source in enumerate((x, h)):
@@ -64,13 +74,49 @@ def tile_forcedgpulstmcell_kernel(
                 raw[s, mp] = acts.tile([P, 2, FEATURES], BF16, name="raw_%d_%d" % (s, mp))
                 nc.sync.dma_start(out=raw[s, mp][:], in_=by_pair[mp])
 
-        bias_rows = const.tile([P, N_TILE], BF16)
-        nc.vector.memset(bias_rows[:], 0.0)
+        w_planes = []
         for q in range(GATES):
-            nc.scalar.dma_start(
-                out=bias_rows[N_HALVES * q : N_HALVES * (q + 1), :],
-                in_=gate_inputs[q][2].rearrange("(j n) -> j n", j=N_HALVES),
+            planes = weights.tile([P, HIDDEN], U8, name="w_planes_%d" % q, align_bytes=64)
+            nc.vector.memset(planes[:].bitcast(I32), 0)
+            w_planes.append(planes)
+
+        def load_scales(q, s):
+            for quadrant in range(4):
+                first = 32 * quadrant + GROUPS * PLANE_ROWS * s
+                nc.sync.dma_start(
+                    out=w_planes[q][first : first + GROUPS * PLANE_ROWS, :].bitcast(I32),
+                    in_=gate_inputs[q][1][s][
+                        :, PLANE_ROWS * quadrant : PLANE_ROWS * (quadrant + 1), :
+                    ].bitcast(I32),
+                )
+
+        w_words = {}
+
+        def load_words(q, s, j):
+            w_words[q, s, j] = weights.tile(
+                [P, GROUPS, N_TILE], U32, name="w_words_%d_%d_%d" % (q, s, j), align_bytes=64
             )
+            by_bytes = gate_inputs[q][0][s].rearrange("g p n t -> p g (n t)")
+            nc.sync.dma_start(
+                out=w_words[q, s, j][:].bitcast(I32),
+                in_=by_bytes[:, :, PACK * N_TILE * j : PACK * N_TILE * (j + 1)].bitcast(I32),
+            )
+
+        c_half = []
+        c_by_tile = c.rearrange("(m p) n -> p m n", p=P)
+        for j in range(N_HALVES):
+            for q in range(GATES):
+                if q == GATE_F:
+                    c_half.append(acts.tile([P, M_TILES, N_TILE], BF16, name="c_half_%d" % j))
+                    nc.sync.dma_start(
+                        out=c_half[j][:], in_=c_by_tile[:, :, N_TILE * j : N_TILE * (j + 1)]
+                    )
+                if j == 0:
+                    load_scales(q, 0)
+                load_words(q, 0, j)
+                load_words(q, 1, j)
+                if j == 0:
+                    load_scales(q, 1)
 
         warm = const.tile([P, 1], F32)
         nc.vector.memset(warm[:], 0.0)
@@ -80,53 +126,6 @@ def tile_forcedgpulstmcell_kernel(
         make_identity(nc, ident_bf16[:])
         ident_f32 = const.tile([P, P], F32)
         make_identity(nc, ident_f32[:])
-
-        w_planes = []
-        for q in range(GATES):
-            planes = weights.tile([P, HIDDEN], U8, name="w_planes_%d" % q, align_bytes=64)
-            nc.vector.memset(planes[:].bitcast(I32), 0)
-            w_planes.append(planes)
-
-        def load_scales(q):
-            for s in range(SOURCES):
-                for quadrant in range(4):
-                    first = 32 * quadrant + GROUPS * PLANE_ROWS * s
-                    nc.sync.dma_start(
-                        out=w_planes[q][first : first + GROUPS * PLANE_ROWS, :].bitcast(I32),
-                        in_=gate_inputs[q][1][s][
-                            :, PLANE_ROWS * quadrant : PLANE_ROWS * (quadrant + 1), :
-                        ].bitcast(I32),
-                    )
-
-        w_words = {}
-
-        def load_words(q, j):
-            for s in range(SOURCES):
-                for g in range(GROUPS):
-                    k = GROUPS * s + g
-                    w_words[q, k, j] = weights.tile(
-                        [P, N_TILE], U32, name="w_words_%d_%d_%d" % (q, k, j), align_bytes=64
-                    )
-                    by_bytes = gate_inputs[q][0][s][g].rearrange("p n t -> p (n t)")
-                    nc.sync.dma_start(
-                        out=w_words[q, k, j][:].bitcast(I32),
-                        in_=by_bytes[:, PACK * N_TILE * j : PACK * N_TILE * (j + 1)].bitcast(I32),
-                    )
-
-        c_half = []
-        c_by_tile = c.rearrange("(m p) n -> p m n", p=P)
-
-        def load_c(j):
-            c_half.append(acts.tile([P, M_TILES, N_TILE], BF16, name="c_half_%d" % j))
-            nc.sync.dma_start(out=c_half[j][:], in_=c_by_tile[:, :, N_TILE * j : N_TILE * (j + 1)])
-
-        for j in range(N_HALVES):
-            for q in range(GATES):
-                if j == 0:
-                    load_scales(q)
-                if q == GATE_F:
-                    load_c(j)
-                load_words(q, j)
 
         bias_all = const.tile([P, GATES, N_HALVES, N_TILE], BF16)
         for q in range(GATES):
@@ -180,64 +179,74 @@ def tile_forcedgpulstmcell_kernel(
                         in_=grouped_flat,
                     )
 
-        def gate_values(q, j, mp, func):
-            values = []
-            sums = [psum.tile([P, N_TILE], F32, tag="bank", name="sums_%d" % m) for m in range(2)]
-            for k in range(PASSES):
-                for m in range(2):
-                    nc.tensor.matmul_mx(
-                        out=sums[m][:],
-                        lhsT=z_codes[k, mp][:, P * m : P * (m + 1)].bitcast(FP8X4),
-                        lhsT_scale=z_scales[k, mp][:, P * m : P * (m + 1)],
-                        rhs=w_words[q, k, j][:].bitcast(FP8X4),
-                        rhs_scale=w_planes[q][PLANE_ROWS * k : P, N_TILE * j : N_TILE * (j + 1)],
-                        start=(k == 0),
-                        stop=(k == PASSES - 1),
-                    )
-            for m in range(2):
-                value = work.tile([P, N_TILE], F32, tag="gate_%d" % q, name="gate_%d" % q)
-                nc.vector.tensor_tensor(
-                    out=value[:], in0=sums[m][:], in1=bias_all[:, q, j, :], op=ADD
+        def gate_sums(q, j):
+            sums = [
+                psum.tile([P, N_TILE], F32, tag="bank", name="sums_%d" % m) for m in range(M_TILES)
+            ]
+            if j == 0 and q == GATE_I:
+                pass_order = [(k, m) for k in range(PASSES) for m in range(M_TILES)]
+            else:
+                pass_order = [(k, m) for m in range(M_TILES) for k in range(PASSES)]
+            for k, m in pass_order:
+                rows = slice(P * (m % 2), P * (m % 2 + 1))
+                nc.tensor.matmul_mx(
+                    out=sums[m][:],
+                    lhsT=z_codes[k, m // 2][:, rows].bitcast(FP8X4),
+                    lhsT_scale=z_scales[k, m // 2][:, rows],
+                    rhs=w_words[q, k // GROUPS, j][:, k % GROUPS, :].bitcast(FP8X4),
+                    rhs_scale=w_planes[q][PLANE_ROWS * k : P, N_TILE * j : N_TILE * (j + 1)],
+                    start=(k == 0),
+                    stop=(k == PASSES - 1),
                 )
-                nc.scalar.activation(out=value[:], in_=value[:], func=func)
-                values.append(value)
-            return values
+            return sums
+
+        def gate_value(q, j, bank, func):
+            value = work.tile([P, N_TILE], F32, tag="gate_%d" % q, name="gate_%d" % q)
+            nc.vector.tensor_tensor(out=value[:], in0=bank[:], in1=bias_all[:, q, j, :], op=ADD)
+            nc.scalar.activation(out=value[:], in_=value[:], func=func)
+            return value
 
         for j in range(N_HALVES):
             columns = slice(N_TILE * j, N_TILE * (j + 1))
-            gate_i = []
-            for mp in range(M_PAIRS):
-                gate_i.extend(gate_values(GATE_I, j, mp, SIGMOID))
-            new_part = []
-            for mp in range(M_PAIRS):
-                gate_g = gate_values(GATE_G, j, mp, TANH)
-                for m in range(2):
-                    new_part.append(work.tile([P, N_TILE], F32, tag="new_part", name="new_part"))
-                    nc.gpsimd.tensor_tensor(
-                        out=new_part[2 * mp + m][:], in0=gate_i[2 * mp + m][:], in1=gate_g[m][:], op=MULT
-                    )
-            tanh_c = []
-            for mp in range(M_PAIRS):
-                gate_f = gate_values(GATE_F, j, mp, SIGMOID)
-                for m in range(2):
-                    tile_rows = slice(P * (2 * mp + m), P * (2 * mp + m + 1))
-                    kept_part = work.tile([P, N_TILE], F32, tag="kept_part")
-                    nc.gpsimd.tensor_tensor(
-                        out=kept_part[:], in0=gate_f[m][:], in1=c_half[j][:, 2 * mp + m, :], op=MULT
-                    )
-                    c_new = work.tile([P, N_TILE], F32, tag="c_new")
-                    nc.vector.tensor_tensor(
-                        out=c_new[:], in0=kept_part[:], in1=new_part[2 * mp + m][:], op=ADD
-                    )
-                    nc.sync.dma_start(out=out_1[tile_rows, columns], in_=c_new[:])
-                    tanh_c.append(work.tile([P, N_TILE], F32, tag="tanh_c", name="tanh_c"))
-                    nc.scalar.activation(out=tanh_c[2 * mp + m][:], in_=c_new[:], func=TANH)
-            for mp in range(M_PAIRS):
-                gate_o = gate_values(GATE_O, j, mp, SIGMOID)
-                for m in range(2):
-                    tile_rows = slice(P * (2 * mp + m), P * (2 * mp + m + 1))
-                    h_new = work.tile([P, N_TILE], F32, tag="h_new")
-                    nc.vector.tensor_tensor(
-                        out=h_new[:], in0=gate_o[m][:], in1=tanh_c[2 * mp + m][:], op=MULT
-                    )
-                    nc.sync.dma_start(out=out_0[tile_rows, columns], in_=h_new[:])
+            new_part, kept_part, tanh_c, gate_o = [], [], [], []
+
+            def finish_cell(m):
+                c_new = work.tile([P, N_TILE], F32, tag="c_new")
+                nc.vector.tensor_tensor(
+                    out=c_new[:], in0=kept_part[m][:], in1=new_part[m][:], op=ADD
+                )
+                nc.sync.dma_start(out=out_1[P * m : P * (m + 1), columns], in_=c_new[:])
+                tanh_c.append(work.tile([P, N_TILE], F32, tag="tanh_c", name="tanh_c"))
+                nc.scalar.activation(out=tanh_c[m][:], in_=c_new[:], func=TANH)
+
+            def finish_hidden(m):
+                engine = nc.gpsimd if m < M_TILES - LAG else nc.vector
+                h_new = work.tile([P, N_TILE], F32, tag="h_new")
+                engine.tensor_tensor(out=h_new[:], in0=gate_o[m][:], in1=tanh_c[m][:], op=MULT)
+                nc.sync.dma_start(out=out_0[P * m : P * (m + 1), columns], in_=h_new[:])
+
+            sums = gate_sums(GATE_I, j)
+            gate_i = [gate_value(GATE_I, j, sums[m], SIGMOID) for m in range(M_TILES)]
+            sums = gate_sums(GATE_G, j)
+            for m in range(M_TILES):
+                gate_g = gate_value(GATE_G, j, sums[m], TANH)
+                new_part.append(work.tile([P, N_TILE], F32, tag="new_part", name="new_part"))
+                nc.gpsimd.tensor_tensor(out=new_part[m][:], in0=gate_i[m][:], in1=gate_g[:], op=MULT)
+            sums = gate_sums(GATE_F, j)
+            for m in range(M_TILES):
+                gate_f = gate_value(GATE_F, j, sums[m], SIGMOID)
+                kept_part.append(work.tile([P, N_TILE], F32, tag="kept_part", name="kept_part"))
+                nc.gpsimd.tensor_tensor(
+                    out=kept_part[m][:], in0=gate_f[:], in1=c_half[j][:, m, :], op=MULT
+                )
+                if m >= LAG:
+                    finish_cell(m - LAG)
+            sums = gate_sums(GATE_O, j)
+            for m in range(M_TILES):
+                gate_o.append(gate_value(GATE_O, j, sums[m], SIGMOID))
+                if m < LAG:
+                    finish_cell(M_TILES - LAG + m)
+                else:
+                    finish_hidden(m - LAG)
+            for m in range(M_TILES - LAG, M_TILES):
+                finish_hidden(m)

@@ -104,8 +104,14 @@ def tile_forcedgpulstmcell_kernel(
 
         c_half = []
         c_by_tile = c.rearrange("(m p) n -> p m n", p=P)
+        load_scales(GATE_I, 0)
+        load_words(GATE_I, 0, 0)
+        load_words(GATE_I, 1, 0)
+        load_scales(GATE_I, 1)
+        load_words(GATE_I, 0, 1)
+        load_words(GATE_I, 1, 1)
         for j in range(N_HALVES):
-            for q in range(GATES):
+            for q in (GATE_G, GATE_F, GATE_O):
                 if q == GATE_F:
                     c_half.append(acts.tile([P, M_TILES, N_TILE], BF16, name="c_half_%d" % j))
                     nc.sync.dma_start(
@@ -201,10 +207,19 @@ def tile_forcedgpulstmcell_kernel(
             return sums
 
         def gate_value(q, j, bank, func):
-            value = work.tile([P, N_TILE], F32, tag="gate_%d" % q, name="gate_%d" % q)
+            value = work.tile(
+                [P, N_TILE], F32, tag="gate_%d" % q, name="gate_%d" % q,
+                bufs=(N_HALVES * M_TILES if q == GATE_I else M_TILES),
+            )
             nc.vector.tensor_tensor(out=value[:], in0=bank[:], in1=bias_all[:, q, j, :], op=ADD)
             nc.scalar.activation(out=value[:], in_=value[:], func=func)
             return value
+
+        gate_i = {}
+        for j in range(N_HALVES):
+            sums = gate_sums(GATE_I, j)
+            for m in range(M_TILES):
+                gate_i[j, m] = gate_value(GATE_I, j, sums[m], SIGMOID)
 
         for j in range(N_HALVES):
             columns = slice(N_TILE * j, N_TILE * (j + 1))
@@ -225,13 +240,11 @@ def tile_forcedgpulstmcell_kernel(
                 engine.tensor_tensor(out=h_new[:], in0=gate_o[m][:], in1=tanh_c[m][:], op=MULT)
                 nc.sync.dma_start(out=out_0[P * m : P * (m + 1), columns], in_=h_new[:])
 
-            sums = gate_sums(GATE_I, j)
-            gate_i = [gate_value(GATE_I, j, sums[m], SIGMOID) for m in range(M_TILES)]
             sums = gate_sums(GATE_G, j)
             for m in range(M_TILES):
                 gate_g = gate_value(GATE_G, j, sums[m], TANH)
                 new_part.append(work.tile([P, N_TILE], F32, tag="new_part", name="new_part"))
-                nc.gpsimd.tensor_tensor(out=new_part[m][:], in0=gate_i[m][:], in1=gate_g[:], op=MULT)
+                nc.gpsimd.tensor_tensor(out=new_part[m][:], in0=gate_i[j, m][:], in1=gate_g[:], op=MULT)
             sums = gate_sums(GATE_F, j)
             for m in range(M_TILES):
                 gate_f = gate_value(GATE_F, j, sums[m], SIGMOID)

@@ -26,7 +26,7 @@ M_PAIRS = M_TILES // 2
 N_TILE = 512
 N_HALVES = HIDDEN // N_TILE
 GATES = 4
-LAG = 2
+LAG = 1
 PLANE_ROWS = 4
 
 FLOPS = 2 * BATCH * (SOURCES * FEATURES) * (GATES * HIDDEN)
@@ -104,14 +104,8 @@ def tile_forcedgpulstmcell_kernel(
 
         c_half = []
         c_by_tile = c.rearrange("(m p) n -> p m n", p=P)
-        load_scales(GATE_I, 0)
-        load_words(GATE_I, 0, 0)
-        load_words(GATE_I, 1, 0)
-        load_scales(GATE_I, 1)
-        load_words(GATE_I, 0, 1)
-        load_words(GATE_I, 1, 1)
         for j in range(N_HALVES):
-            for q in (GATE_G, GATE_F, GATE_O):
+            for q in range(GATES):
                 if q == GATE_F:
                     c_half.append(acts.tile([P, M_TILES, N_TILE], BF16, name="c_half_%d" % j))
                     nc.sync.dma_start(
@@ -207,52 +201,50 @@ def tile_forcedgpulstmcell_kernel(
             return sums
 
         def gate_value(q, j, bank, func):
-            value = work.tile(
-                [P, N_TILE], F32, tag="gate_%d" % q, name="gate_%d" % q,
-                bufs=(N_HALVES * M_TILES if q == GATE_I else M_TILES),
-            )
+            value = work.tile([P, N_TILE], F32, tag="gate_%d" % q, name="gate_%d" % q)
             nc.vector.tensor_tensor(out=value[:], in0=bank[:], in1=bias_all[:, q, j, :], op=ADD)
             nc.scalar.activation(out=value[:], in_=value[:], func=func)
             return value
 
-        gate_i = {}
-        for j in range(N_HALVES):
-            sums = gate_sums(GATE_I, j)
-            for m in range(M_TILES):
-                gate_i[j, m] = gate_value(GATE_I, j, sums[m], SIGMOID)
-
         for j in range(N_HALVES):
             columns = slice(N_TILE * j, N_TILE * (j + 1))
-            new_part, kept_part, tanh_c, gate_o = [], [], [], []
+            gate_g, gate_f, gate_o, new_part, tanh_c = [], [], [], [], []
+
+            def form_new_part(m):
+                new_part.append(work.tile([P, N_TILE], F32, tag="new_part", name="new_part"))
+                nc.vector.tensor_tensor(
+                    out=new_part[m][:], in0=gate_i[m][:], in1=gate_g[m][:], op=MULT
+                )
 
             def finish_cell(m):
-                c_new = work.tile([P, N_TILE], F32, tag="c_new")
+                kept_part = work.tile([P, N_TILE], F32, tag="kept_part")
                 nc.vector.tensor_tensor(
-                    out=c_new[:], in0=kept_part[m][:], in1=new_part[m][:], op=ADD
+                    out=kept_part[:], in0=gate_f[m][:], in1=c_half[j][:, m, :], op=MULT
                 )
+                c_new = work.tile([P, N_TILE], F32, tag="c_new")
+                nc.vector.tensor_tensor(out=c_new[:], in0=kept_part[:], in1=new_part[m][:], op=ADD)
                 nc.sync.dma_start(out=out_1[P * m : P * (m + 1), columns], in_=c_new[:])
                 tanh_c.append(work.tile([P, N_TILE], F32, tag="tanh_c", name="tanh_c"))
                 nc.scalar.activation(out=tanh_c[m][:], in_=c_new[:], func=TANH)
 
             def finish_hidden(m):
-                engine = nc.gpsimd if m < M_TILES - LAG else nc.vector
                 h_new = work.tile([P, N_TILE], F32, tag="h_new")
-                engine.tensor_tensor(out=h_new[:], in0=gate_o[m][:], in1=tanh_c[m][:], op=MULT)
+                nc.vector.tensor_tensor(out=h_new[:], in0=gate_o[m][:], in1=tanh_c[m][:], op=MULT)
                 nc.sync.dma_start(out=out_0[P * m : P * (m + 1), columns], in_=h_new[:])
 
+            sums = gate_sums(GATE_I, j)
+            gate_i = [gate_value(GATE_I, j, sums[m], SIGMOID) for m in range(M_TILES)]
             sums = gate_sums(GATE_G, j)
             for m in range(M_TILES):
-                gate_g = gate_value(GATE_G, j, sums[m], TANH)
-                new_part.append(work.tile([P, N_TILE], F32, tag="new_part", name="new_part"))
-                nc.gpsimd.tensor_tensor(out=new_part[m][:], in0=gate_i[j, m][:], in1=gate_g[:], op=MULT)
+                gate_g.append(gate_value(GATE_G, j, sums[m], TANH))
+                if m >= LAG:
+                    form_new_part(m - LAG)
             sums = gate_sums(GATE_F, j)
             for m in range(M_TILES):
-                gate_f = gate_value(GATE_F, j, sums[m], SIGMOID)
-                kept_part.append(work.tile([P, N_TILE], F32, tag="kept_part", name="kept_part"))
-                nc.gpsimd.tensor_tensor(
-                    out=kept_part[m][:], in0=gate_f[:], in1=c_half[j][:, m, :], op=MULT
-                )
-                if m >= LAG:
+                gate_f.append(gate_value(GATE_F, j, sums[m], SIGMOID))
+                if m < LAG:
+                    form_new_part(M_TILES - LAG + m)
+                else:
                     finish_cell(m - LAG)
             sums = gate_sums(GATE_O, j)
             for m in range(M_TILES):

@@ -26,7 +26,7 @@ M_PAIRS = M_TILES // 2
 N_TILE = 512
 N_HALVES = HIDDEN // N_TILE
 GATES = 4
-LAG = 1
+LAG = 2
 PLANE_ROWS = 4
 
 FLOPS = 2 * BATCH * (SOURCES * FEATURES) * (GATES * HIDDEN)
@@ -180,13 +180,12 @@ def tile_forcedgpulstmcell_kernel(
                     )
 
         def gate_sums(q, j):
-            sums = [
-                psum.tile([P, N_TILE], F32, tag="bank", name="sums_%d" % m) for m in range(M_TILES)
-            ]
+            tiles = range(M_TILES)
+            sums = [psum.tile([P, N_TILE], F32, tag="bank", name="sums_%d" % m) for m in tiles]
             if j == 0 and q == GATE_I:
-                pass_order = [(k, m) for k in range(PASSES) for m in range(M_TILES)]
+                pass_order = [(k, m) for k in range(PASSES) for m in tiles]
             else:
-                pass_order = [(k, m) for m in range(M_TILES) for k in range(PASSES)]
+                pass_order = [(k, m) for m in tiles for k in range(PASSES)]
             for k, m in pass_order:
                 rows = slice(P * (m % 2), P * (m % 2 + 1))
                 nc.tensor.matmul_mx(
@@ -200,58 +199,69 @@ def tile_forcedgpulstmcell_kernel(
                 )
             return sums
 
-        def gate_value(q, j, bank, func):
-            value = work.tile([P, N_TILE], F32, tag="gate_%d" % q, name="gate_%d" % q)
-            nc.vector.tensor_tensor(out=value[:], in0=bank[:], in1=bias_all[:, q, j, :], op=ADD)
-            nc.scalar.activation(out=value[:], in_=value[:], func=func)
-            return value
+        gate = {}
+        new_part = {}
+        kept_part = {}
+        tanh_c = {}
 
+        def form_new_part(j, m):
+            new_part[j, m] = work.tile([P, N_TILE], F32, tag="new_part", name="new_part")
+            nc.vector.tensor_tensor(
+                out=new_part[j, m][:], in0=gate[GATE_I, j, m][:], in1=gate[GATE_G, j, m][:], op=MULT
+            )
+
+        def form_kept_part(j, m):
+            kept_part[j, m] = work.tile([P, N_TILE], F32, tag="kept_part", name="kept_part")
+            nc.vector.tensor_tensor(
+                out=kept_part[j, m][:], in0=gate[GATE_F, j, m][:], in1=c_half[j][:, m, :], op=MULT
+            )
+
+        def finish_cell(j, m):
+            c_new = work.tile([P, N_TILE], F32, tag="c_new")
+            nc.vector.tensor_tensor(
+                out=c_new[:], in0=kept_part[j, m][:], in1=new_part[j, m][:], op=ADD
+            )
+            nc.sync.dma_start(
+                out=out_1[P * m : P * (m + 1), N_TILE * j : N_TILE * (j + 1)], in_=c_new[:]
+            )
+            tanh_c[j, m] = work.tile([P, N_TILE], F32, tag="tanh_c", name="tanh_c")
+            nc.scalar.activation(out=tanh_c[j, m][:], in_=c_new[:], func=TANH)
+
+        def finish_hidden(j, m):
+            h_new = work.tile([P, N_TILE], F32, tag="h_new")
+            nc.vector.tensor_tensor(
+                out=h_new[:], in0=gate[GATE_O, j, m][:], in1=tanh_c[j, m][:], op=MULT
+            )
+            nc.sync.dma_start(
+                out=out_0[P * m : P * (m + 1), N_TILE * j : N_TILE * (j + 1)], in_=h_new[:]
+            )
+
+        gate_func = {GATE_I: SIGMOID, GATE_G: TANH, GATE_F: SIGMOID, GATE_O: SIGMOID}
+        next_steps = {
+            GATE_I: (),
+            GATE_G: (form_new_part,),
+            GATE_F: (form_kept_part, finish_cell),
+            GATE_O: (finish_hidden,),
+        }
+
+        banks = N_HALVES * GATES * M_TILES
+        later = [[] for b in range(banks + LAG + 2)]
+        b = 0
         for j in range(N_HALVES):
-            columns = slice(N_TILE * j, N_TILE * (j + 1))
-            gate_g, gate_f, gate_o, new_part, tanh_c = [], [], [], [], []
-
-            def form_new_part(m):
-                new_part.append(work.tile([P, N_TILE], F32, tag="new_part", name="new_part"))
-                nc.vector.tensor_tensor(
-                    out=new_part[m][:], in0=gate_i[m][:], in1=gate_g[m][:], op=MULT
-                )
-
-            def finish_cell(m):
-                kept_part = work.tile([P, N_TILE], F32, tag="kept_part")
-                nc.vector.tensor_tensor(
-                    out=kept_part[:], in0=gate_f[m][:], in1=c_half[j][:, m, :], op=MULT
-                )
-                c_new = work.tile([P, N_TILE], F32, tag="c_new")
-                nc.vector.tensor_tensor(out=c_new[:], in0=kept_part[:], in1=new_part[m][:], op=ADD)
-                nc.sync.dma_start(out=out_1[P * m : P * (m + 1), columns], in_=c_new[:])
-                tanh_c.append(work.tile([P, N_TILE], F32, tag="tanh_c", name="tanh_c"))
-                nc.scalar.activation(out=tanh_c[m][:], in_=c_new[:], func=TANH)
-
-            def finish_hidden(m):
-                h_new = work.tile([P, N_TILE], F32, tag="h_new")
-                nc.vector.tensor_tensor(out=h_new[:], in0=gate_o[m][:], in1=tanh_c[m][:], op=MULT)
-                nc.sync.dma_start(out=out_0[P * m : P * (m + 1), columns], in_=h_new[:])
-
-            sums = gate_sums(GATE_I, j)
-            gate_i = [gate_value(GATE_I, j, sums[m], SIGMOID) for m in range(M_TILES)]
-            sums = gate_sums(GATE_G, j)
-            for m in range(M_TILES):
-                gate_g.append(gate_value(GATE_G, j, sums[m], TANH))
-                if m >= LAG:
-                    form_new_part(m - LAG)
-            sums = gate_sums(GATE_F, j)
-            for m in range(M_TILES):
-                gate_f.append(gate_value(GATE_F, j, sums[m], SIGMOID))
-                if m < LAG:
-                    form_new_part(M_TILES - LAG + m)
-                else:
-                    finish_cell(m - LAG)
-            sums = gate_sums(GATE_O, j)
-            for m in range(M_TILES):
-                gate_o.append(gate_value(GATE_O, j, sums[m], SIGMOID))
-                if m < LAG:
-                    finish_cell(M_TILES - LAG + m)
-                else:
-                    finish_hidden(m - LAG)
-            for m in range(M_TILES - LAG, M_TILES):
-                finish_hidden(m)
+            for q in (GATE_I, GATE_G, GATE_F, GATE_O):
+                sums = gate_sums(q, j)
+                for m in range(M_TILES):
+                    value = work.tile([P, N_TILE], F32, tag="gate_%d" % q, name="gate_%d" % q)
+                    nc.vector.tensor_tensor(
+                        out=value[:], in0=sums[m][:], in1=bias_all[:, q, j, :], op=ADD
+                    )
+                    nc.scalar.activation(out=value[:], in_=value[:], func=gate_func[q])
+                    gate[q, j, m] = value
+                    for n, step in enumerate(next_steps[q]):
+                        later[b + LAG + n].append((step, j, m))
+                    for step, step_j, step_m in later[b]:
+                        step(step_j, step_m)
+                    b += 1
+        for steps in later[banks:]:
+            for step, step_j, step_m in steps:
+                step(step_j, step_m)

@@ -50,35 +50,40 @@ def tile_forcedgpulstmcell_kernel(
         ((weight_io_words, weight_ho_words), (weight_io_scales, weight_ho_scales), bias_o),
     )
     GATE_I, GATE_G, GATE_F, GATE_O = 0, 1, 2, 3
+    units = ((GATE_I, 0), (GATE_G, 0), (GATE_F, 0), (GATE_O, 0), (GATE_I, 1), (GATE_G, 1), (GATE_F, 1), (GATE_O, 1))
 
     with ExitStack() as ctx:
         const = ctx.enter_context(tc.tile_pool(name="const", bufs=1))
         acts = ctx.enter_context(tc.tile_pool(name="acts", bufs=1))
         weights = ctx.enter_context(tc.tile_pool(name="weights", bufs=1))
         work = ctx.enter_context(tc.tile_pool(name="work", bufs=M_TILES))
-        psum = ctx.enter_context(tc.psum_pool(name="psum", bufs=8))
+        psum = ctx.enter_context(tc.psum_pool(name="psum", bufs=2 * M_TILES))
+        bank_sets = ("bank", "bank")
         ctx.enter_context(tc.manual_schedule())
 
         bias_rows = const.tile([P, N_TILE], BF16)
         nc.vector.memset(bias_rows[:], 0.0)
-        for q in range(GATES):
-            nc.sync.dma_start(
-                out=bias_rows[N_HALVES * q : N_HALVES * (q + 1), :],
-                in_=gate_inputs[q][2].rearrange("(j n) -> j n", j=N_HALVES),
-            )
-
-        raw = {}
-        for s, source in enumerate((x, h)):
-            by_pair = source.rearrange("(mp m p) k -> mp p m k", m=2, p=P)
-            for mp in range(M_PAIRS):
-                raw[s, mp] = acts.tile([P, 2, FEATURES], BF16, name="raw_%d_%d" % (s, mp))
-                nc.sync.dma_start(out=raw[s, mp][:], in_=by_pair[mp])
-
         w_planes = []
         for q in range(GATES):
             planes = weights.tile([P, HIDDEN], U8, name="w_planes_%d" % q, align_bytes=64)
             nc.vector.memset(planes[:].bitcast(I32), 0)
             w_planes.append(planes)
+        raw = {}
+        w_words = {}
+        c_half = {}
+
+        def load_bias_rows():
+            for q in range(GATES):
+                nc.sync.dma_start(
+                    out=bias_rows[N_HALVES * q : N_HALVES * (q + 1), :],
+                    in_=gate_inputs[q][2].rearrange("(j n) -> j n", j=N_HALVES),
+                )
+
+        def load_source(s):
+            by_pair = (x, h)[s].rearrange("(mp m p) k -> mp p m k", m=2, p=P)
+            for mp in range(M_PAIRS):
+                raw[s, mp] = acts.tile([P, 2, FEATURES], BF16, name="raw_%d_%d" % (s, mp))
+                nc.sync.dma_start(out=raw[s, mp][:], in_=by_pair[mp])
 
         def load_scales(q, s):
             for quadrant in range(4):
@@ -90,8 +95,6 @@ def tile_forcedgpulstmcell_kernel(
                     ].bitcast(I32),
                 )
 
-        w_words = {}
-
         def load_words(q, s, j):
             w_words[q, s, j] = weights.tile(
                 [P, GROUPS, N_TILE], U32, name="w_words_%d_%d_%d" % (q, s, j), align_bytes=64
@@ -102,53 +105,60 @@ def tile_forcedgpulstmcell_kernel(
                 in_=by_bytes[:, :, PACK * N_TILE * j : PACK * N_TILE * (j + 1)].bitcast(I32),
             )
 
-        c_half = []
-        c_by_tile = c.rearrange("(m p) n -> p m n", p=P)
-        for j in range(N_HALVES):
-            for q in range(GATES):
-                if q == GATE_F:
-                    c_half.append(acts.tile([P, M_TILES, N_TILE], BF16, name="c_half_%d" % j))
-                    nc.sync.dma_start(
-                        out=c_half[j][:], in_=c_by_tile[:, :, N_TILE * j : N_TILE * (j + 1)]
-                    )
-                if j == 0:
-                    load_scales(q, 0)
-                load_words(q, 0, j)
-                load_words(q, 1, j)
-                if j == 0:
-                    load_scales(q, 1)
+        def load_c(j):
+            c_half[j] = acts.tile([P, M_TILES, N_TILE], BF16, name="c_half_%d" % j)
+            nc.sync.dma_start(
+                out=c_half[j][:],
+                in_=c.rearrange("(m p) n -> p m n", p=P)[:, :, N_TILE * j : N_TILE * (j + 1)],
+            )
+
+        load_bias_rows()
+        load_source(0)
+        load_source(1)
+        for q, j in units:
+            if q == GATE_F:
+                load_c(j)
+            if j == 0:
+                load_scales(q, 0)
+            load_words(q, 0, j)
+            load_words(q, 1, j)
+            if j == 0:
+                load_scales(q, 1)
 
         warm = const.tile([P, 1], F32)
         nc.vector.memset(warm[:], 0.0)
         nc.scalar.activation(out=warm[:], in_=warm[:], func=SIGMOID)
 
         ident_bf16 = const.tile([P, P], BF16)
-        make_identity(nc, ident_bf16[:])
         ident_f32 = const.tile([P, P], F32)
+        make_identity(nc, ident_bf16[:])
         make_identity(nc, ident_f32[:])
 
         bias_all = const.tile([P, GATES, N_HALVES, N_TILE], BF16)
-        for q in range(GATES):
-            spread = psum.tile([P, N_HALVES, N_TILE], BF16, tag="bank")
-            for j in range(N_HALVES):
-                r = N_HALVES * q + j
-                nc.tensor.matmul(
-                    out=spread[:, j, :],
-                    lhsT=ident_bf16[:, r : r + 1].to_broadcast([P, P]),
-                    rhs=bias_rows[:],
-                    start=True,
-                    stop=True,
-                )
-            nc.scalar.copy(out=bias_all[:, q, :, :], in_=spread[:])
+
+        def spread_biases(bank_set, spread_gates):
+            for q in spread_gates:
+                spread = psum.tile([P, N_HALVES, N_TILE], BF16, tag=bank_set, name="spread")
+                for j in range(N_HALVES):
+                    r = N_HALVES * q + j
+                    nc.tensor.matmul(
+                        out=spread[:, j, :],
+                        lhsT=ident_bf16[:, r : r + 1].to_broadcast([P, P]),
+                        rhs=bias_rows[:],
+                        start=True,
+                        stop=True,
+                    )
+                nc.scalar.copy(out=bias_all[:, q, :, :], in_=spread[:])
 
         z_codes = {}
         z_scales = {}
-        for s in range(SOURCES):
-            for mp in range(M_PAIRS):
+
+        def quantise_source(s, bank_set, pairs):
+            for mp in pairs:
                 words = raw[s, mp][:].bitcast(F32)
                 for g in range(GROUPS):
                     k = GROUPS * s + g
-                    flipped = psum.tile([P, 2, 2 * P], F32, tag="bank")
+                    flipped = psum.tile([P, 2, 2 * P], F32, tag=bank_set, name="flipped")
                     for u in range(2):
                         for m in range(2):
                             nc.tensor.transpose(
@@ -157,7 +167,7 @@ def tile_forcedgpulstmcell_kernel(
                                 ident_f32[:],
                             )
                     grouped = acts.tile(
-                        [P, 2 * P, PACK], BF16, name="grouped_%d_%d" % (k, mp), align_bytes=64
+                        [P, 2 * P, PACK], BF16, name="grouped", tag="grouped", bufs=4, align_bytes=64
                     )
                     grouped_flat = grouped[:].rearrange("p b t -> p (b t)")
                     grouped_words = grouped_flat.bitcast(F32).rearrange("p (b u) -> p b u", u=2)
@@ -179,13 +189,12 @@ def tile_forcedgpulstmcell_kernel(
                         in_=grouped_flat,
                     )
 
-        def gate_sums(q, j):
-            tiles = range(M_TILES)
-            sums = [psum.tile([P, N_TILE], F32, tag="bank", name="sums_%d" % m) for m in tiles]
-            if j == 0 and q == GATE_I:
-                pass_order = [(k, m) for k in range(PASSES) for m in tiles]
-            else:
-                pass_order = [(k, m) for m in tiles for k in range(PASSES)]
+        def open_banks(bank_set):
+            return [
+                psum.tile([P, N_TILE], F32, tag=bank_set, name="sums_%d" % m) for m in range(M_TILES)
+            ]
+
+        def run_passes(sums, q, j, pass_order):
             for k, m in pass_order:
                 rows = slice(P * (m % 2), P * (m % 2 + 1))
                 nc.tensor.matmul_mx(
@@ -197,7 +206,14 @@ def tile_forcedgpulstmcell_kernel(
                     start=(k == 0),
                     stop=(k == PASSES - 1),
                 )
-            return sums
+
+        tiles = range(M_TILES)
+        for step in range(SOURCES * M_PAIRS):
+            spread_biases(bank_sets[0], (step,))
+            quantise_source(step // M_PAIRS, bank_sets[0], (step % M_PAIRS,))
+        first_sums = open_banks(bank_sets[1])
+        run_passes(first_sums, units[0][0], units[0][1], [(k, m) for k in range(PASSES) for m in tiles])
+        first_set = 1
 
         gate = {}
         new_part = {}
@@ -224,12 +240,13 @@ def tile_forcedgpulstmcell_kernel(
             nc.sync.dma_start(
                 out=out_1[P * m : P * (m + 1), N_TILE * j : N_TILE * (j + 1)], in_=c_new[:]
             )
-            tanh_c[j, m] = work.tile([P, N_TILE], F32, tag="tanh_c", name="tanh_c")
+            tanh_c[j, m] = work.tile([P, N_TILE], F32, tag="tanh_c", name="tanh_c", bufs=4)
             nc.scalar.activation(out=tanh_c[j, m][:], in_=c_new[:], func=TANH)
 
         def finish_hidden(j, m):
-            h_new = work.tile([P, N_TILE], F32, tag="h_new")
-            nc.vector.tensor_tensor(
+            h_new = work.tile([P, N_TILE], F32, tag="h_new", bufs=4)
+            engine = nc.gpsimd if False else nc.vector
+            engine.tensor_tensor(
                 out=h_new[:], in0=gate[GATE_O, j, m][:], in1=tanh_c[j, m][:], op=MULT
             )
             nc.sync.dma_start(
@@ -244,24 +261,30 @@ def tile_forcedgpulstmcell_kernel(
             GATE_O: (finish_hidden,),
         }
 
-        banks = N_HALVES * GATES * M_TILES
+        banks = len(units) * M_TILES
         later = [[] for b in range(banks + LAG + 2)]
         b = 0
-        for j in range(N_HALVES):
-            for q in (GATE_I, GATE_G, GATE_F, GATE_O):
-                sums = gate_sums(q, j)
-                for m in range(M_TILES):
-                    value = work.tile([P, N_TILE], F32, tag="gate_%d" % q, name="gate_%d" % q)
-                    nc.vector.tensor_tensor(
-                        out=value[:], in0=sums[m][:], in1=bias_all[:, q, j, :], op=ADD
-                    )
-                    nc.scalar.activation(out=value[:], in_=value[:], func=gate_func[q])
-                    gate[q, j, m] = value
-                    for n, step in enumerate(next_steps[q]):
-                        later[b + LAG + n].append((step, j, m))
-                    for step, step_j, step_m in later[b]:
-                        step(step_j, step_m)
-                    b += 1
+        for u, (q, j) in enumerate(units):
+            if u == 0:
+                sums = first_sums
+            else:
+                sums = open_banks(bank_sets[(first_set + u) % 2])
+                if u < 1:
+                    run_passes(sums, q, j, [(k, m) for k in range(PASSES) for m in tiles])
+                else:
+                    run_passes(sums, q, j, [(k, m) for m in tiles for k in range(PASSES)])
+            for m in tiles:
+                value = work.tile([P, N_TILE], F32, tag="gate_%d" % q, name="gate_%d" % q)
+                nc.vector.tensor_tensor(
+                    out=value[:], in0=sums[m][:], in1=bias_all[:, q, j, :], op=ADD
+                )
+                nc.scalar.activation(out=value[:], in_=value[:], func=gate_func[q])
+                gate[q, j, m] = value
+                for n, step in enumerate(next_steps[q]):
+                    later[b + LAG + n].append((step, j, m))
+                for step, step_j, step_m in later[b]:
+                    step(step_j, step_m)
+                b += 1
         for steps in later[banks:]:
             for step, step_j, step_m in steps:
                 step(step_j, step_m)

@@ -27,6 +27,7 @@ N_TILE = 512
 N_HALVES = HIDDEN // N_TILE
 GATES = 4
 LAG = 2
+SORT_AHEAD = 1
 PLANE_ROWS = 4
 
 FLOPS = 2 * BATCH * (SOURCES * FEATURES) * (GATES * HIDDEN)
@@ -156,6 +157,14 @@ def tile_forcedgpulstmcell_kernel(
         def quantise_source(s, bank_set, pairs):
             for mp in pairs:
                 words = raw[s, mp][:].bitcast(F32)
+                sorted_words = acts.tile(
+                    [P, 2, GROUPS, 2, P], F32, name="sorted_words", tag="sorted_words", bufs=2
+                )
+                for m, copy in enumerate((nc.vector.tensor_copy, nc.scalar.copy)):
+                    copy(
+                        out=sorted_words[:, m, :, :, :],
+                        in_=words[:, m, :].rearrange("p (g w u) -> p g u w", g=GROUPS, u=2),
+                    )
                 for g in range(GROUPS):
                     k = GROUPS * s + g
                     flipped = psum.tile([P, 2, 2 * P], F32, tag=bank_set, name="flipped")
@@ -163,7 +172,7 @@ def tile_forcedgpulstmcell_kernel(
                         for m in range(2):
                             nc.tensor.transpose(
                                 flipped[:, u, P * m : P * (m + 1)],
-                                words[:, m, 2 * P * g + u : 2 * P * (g + 1) : 2],
+                                sorted_words[:, m, g, u, :],
                                 ident_f32[:],
                             )
                     grouped = acts.tile(
@@ -189,6 +198,57 @@ def tile_forcedgpulstmcell_kernel(
                         in_=grouped_flat,
                     )
 
+        sorted_words = {}
+        flipped_banks = {}
+
+        def sort_words(s, mp):
+            words = raw[s, mp][:].bitcast(F32)
+            sorted_words[s, mp] = acts.tile(
+                [P, 2, GROUPS, 2, P], F32, name="sorted_words", tag="sorted_words", bufs=SORT_AHEAD + 1
+            )
+            for m, copy in enumerate((nc.vector.tensor_copy, nc.scalar.copy)):
+                copy(
+                    out=sorted_words[s, mp][:, m, :, :, :],
+                    in_=words[:, m, :].rearrange("p (g w u) -> p g u w", g=GROUPS, u=2),
+                )
+
+        def transpose_pair(s, mp, bank_set):
+            for g in range(GROUPS):
+                flipped = psum.tile([P, 2, 2 * P], F32, tag=bank_set, name="flipped")
+                for u in range(2):
+                    for m in range(2):
+                        nc.tensor.transpose(
+                            flipped[:, u, P * m : P * (m + 1)],
+                            sorted_words[s, mp][:, m, g, u, :],
+                            ident_f32[:],
+                        )
+                flipped_banks[s, mp, g] = flipped
+
+        def quantise_pair(s, mp):
+            grouped_flat = {}
+            for g, copy in enumerate((nc.vector.tensor_copy, nc.scalar.copy)):
+                grouped = acts.tile(
+                    [P, 2 * P, PACK], BF16, name="grouped", tag="grouped", bufs=4, align_bytes=64
+                )
+                grouped_flat[g] = grouped[:].rearrange("p b t -> p (b t)")
+                copy(
+                    out=grouped_flat[g].bitcast(F32).rearrange("p (b u) -> p b u", u=2),
+                    in_=flipped_banks[s, mp, g][:].rearrange("p u b -> p b u"),
+                )
+            for g in range(GROUPS):
+                k = GROUPS * s + g
+                z_codes[k, mp] = acts.tile(
+                    [P, 2 * P], U32, name="z_codes_%d_%d" % (k, mp), align_bytes=64
+                )
+                z_scales[k, mp] = acts.tile(
+                    [P, 2 * P], U8, name="z_scales_%d_%d" % (k, mp), align_bytes=64
+                )
+                nc.vector.quantize_mx(
+                    out=z_codes[k, mp][:].bitcast(FP8X4),
+                    scales=z_scales[k, mp][:],
+                    in_=grouped_flat[g],
+                )
+
         def open_banks(bank_set):
             return [
                 psum.tile([P, N_TILE], F32, tag=bank_set, name="sums_%d" % m) for m in range(M_TILES)
@@ -208,9 +268,15 @@ def tile_forcedgpulstmcell_kernel(
                 )
 
         tiles = range(M_TILES)
-        for step in range(SOURCES * M_PAIRS):
+        steps = SOURCES * M_PAIRS
+        for step in range(SORT_AHEAD):
+            sort_words(step // M_PAIRS, step % M_PAIRS)
+        for step in range(steps):
             spread_biases(bank_sets[0], (step,))
-            quantise_source(step // M_PAIRS, bank_sets[0], (step % M_PAIRS,))
+            transpose_pair(step // M_PAIRS, step % M_PAIRS, bank_sets[0])
+            if step + SORT_AHEAD < steps:
+                sort_words((step + SORT_AHEAD) // M_PAIRS, (step + SORT_AHEAD) % M_PAIRS)
+            quantise_pair(step // M_PAIRS, step % M_PAIRS)
         first_sums = open_banks(bank_sets[1])
         run_passes(first_sums, units[0][0], units[0][1], [(k, m) for k in range(PASSES) for m in tiles])
         first_set = 1

@@ -64,11 +64,13 @@ def tile_forcedgpulstmcell_kernel(
 
         bias_rows = const.tile([P, N_TILE], BF16)
         nc.vector.memset(bias_rows[:], 0.0)
-        w_planes = []
+        w_planes = {}
         for q in range(GATES):
-            planes = weights.tile([P, HIDDEN], U8, name="w_planes_%d" % q, align_bytes=64)
-            nc.vector.memset(planes[:].bitcast(I32), 0)
-            w_planes.append(planes)
+            for s in range(SOURCES):
+                w_planes[q, s] = weights.tile(
+                    [P, HIDDEN], U8, name="w_planes_%d_%d" % (q, s), align_bytes=64
+                )
+                nc.vector.memset(w_planes[q, s][:].bitcast(I32), 0)
         raw = {}
         w_words = {}
         c_half = {}
@@ -80,17 +82,20 @@ def tile_forcedgpulstmcell_kernel(
                     in_=gate_inputs[q][2].rearrange("(j n) -> j n", j=N_HALVES),
                 )
 
-        def load_source(s):
+        def load_pair(s, mp):
             by_pair = (x, h)[s].rearrange("(mp m p) k -> mp p m k", m=2, p=P)
+            raw[s, mp] = acts.tile([P, 2, FEATURES], BF16, name="raw_%d_%d" % (s, mp))
+            nc.sync.dma_start(out=raw[s, mp][:], in_=by_pair[mp])
+
+        def load_source(s):
             for mp in range(M_PAIRS):
-                raw[s, mp] = acts.tile([P, 2, FEATURES], BF16, name="raw_%d_%d" % (s, mp))
-                nc.sync.dma_start(out=raw[s, mp][:], in_=by_pair[mp])
+                load_pair(s, mp)
 
         def load_scales(q, s):
             for quadrant in range(4):
-                first = 32 * quadrant + GROUPS * PLANE_ROWS * s
+                first = 32 * quadrant
                 nc.sync.dma_start(
-                    out=w_planes[q][first : first + GROUPS * PLANE_ROWS, :].bitcast(I32),
+                    out=w_planes[q, s][first : first + GROUPS * PLANE_ROWS, :].bitcast(I32),
                     in_=gate_inputs[q][1][s][
                         :, PLANE_ROWS * quadrant : PLANE_ROWS * (quadrant + 1), :
                     ].bitcast(I32),
@@ -113,10 +118,17 @@ def tile_forcedgpulstmcell_kernel(
                 in_=c.rearrange("(m p) n -> p m n", p=P)[:, :, N_TILE * j : N_TILE * (j + 1)],
             )
 
+        first_q, first_j = units[0]
         load_bias_rows()
-        load_source(0)
-        load_source(1)
-        for q, j in units:
+        load_pair(0, 0)
+        load_pair(0, 1)
+        load_pair(1, 0)
+        load_scales(first_q, 0)
+        load_words(first_q, 0, first_j)
+        load_pair(1, 1)
+        load_scales(first_q, 1)
+        load_words(first_q, 1, first_j)
+        for q, j in units[1:]:
             if q == GATE_F:
                 load_c(j)
             if j == 0:
@@ -206,11 +218,10 @@ def tile_forcedgpulstmcell_kernel(
             sorted_words[s, mp] = acts.tile(
                 [P, 2, GROUPS, 2, P], F32, name="sorted_words", tag="sorted_words", bufs=SORT_AHEAD + 1
             )
-            for m, copy in enumerate((nc.vector.tensor_copy, nc.scalar.copy)):
-                copy(
-                    out=sorted_words[s, mp][:, m, :, :, :],
-                    in_=words[:, m, :].rearrange("p (g w u) -> p g u w", g=GROUPS, u=2),
-                )
+            nc.vector.tensor_copy(
+                out=sorted_words[s, mp][:].rearrange("p m g u w -> p (m g) u w"),
+                in_=words.rearrange("p m (g w u) -> p (m g) u w", g=GROUPS, u=2),
+            )
 
         def transpose_pair(s, mp, bank_set):
             for g in range(GROUPS):
@@ -249,56 +260,73 @@ def tile_forcedgpulstmcell_kernel(
                     in_=grouped_flat[g],
                 )
 
-        def open_banks(bank_set):
+        whole_tiles = [(m, 0, N_TILE) for m in range(M_TILES)]
+        unit_pieces = [whole_tiles for unit in units]
+
+        def open_banks(bank_set, pieces):
             return [
-                psum.tile([P, N_TILE], F32, tag=bank_set, name="sums_%d" % m) for m in range(M_TILES)
+                psum.tile([P, width], F32, tag=bank_set, name="sums_%d_%d" % (m, first))
+                for m, first, width in pieces
             ]
 
-        def run_passes(sums, q, j, pass_order):
-            for k, m in pass_order:
+        def run_passes(sums, pieces, q, j, pass_order):
+            for k, n in pass_order:
+                m, first, width = pieces[n]
                 rows = slice(P * (m % 2), P * (m % 2 + 1))
+                columns = slice(N_TILE * j + first, N_TILE * j + first + width)
                 nc.tensor.matmul_mx(
-                    out=sums[m][:],
+                    out=sums[n][:],
                     lhsT=z_codes[k, m // 2][:, rows].bitcast(FP8X4),
                     lhsT_scale=z_scales[k, m // 2][:, rows],
-                    rhs=w_words[q, k // GROUPS, j][:, k % GROUPS, :].bitcast(FP8X4),
-                    rhs_scale=w_planes[q][PLANE_ROWS * k : P, N_TILE * j : N_TILE * (j + 1)],
+                    rhs=w_words[q, k // GROUPS, j][:, k % GROUPS, first : first + width].bitcast(FP8X4),
+                    rhs_scale=w_planes[q, k // GROUPS][PLANE_ROWS * (k % GROUPS) : P, columns],
                     start=(k == 0),
                     stop=(k == PASSES - 1),
                 )
 
         tiles = range(M_TILES)
-        steps = SOURCES * M_PAIRS
-        for step in range(SORT_AHEAD):
-            sort_words(step // M_PAIRS, step % M_PAIRS)
-        for step in range(steps):
-            spread_biases(bank_sets[0], (step,))
-            transpose_pair(step // M_PAIRS, step % M_PAIRS, bank_sets[0])
-            if step + SORT_AHEAD < steps:
-                sort_words((step + SORT_AHEAD) // M_PAIRS, (step + SORT_AHEAD) % M_PAIRS)
-            quantise_pair(step // M_PAIRS, step % M_PAIRS)
-        first_sums = open_banks(bank_sets[1])
-        run_passes(first_sums, units[0][0], units[0][1], [(k, m) for k in range(PASSES) for m in tiles])
-        first_set = 1
+        sort_words(0, 0)
+        spread_biases(bank_sets[0], (GATE_I, GATE_G))
+        transpose_pair(0, 0, bank_sets[0])
+        sort_words(0, 1)
+        quantise_pair(0, 0)
+        transpose_pair(0, 1, bank_sets[0])
+        sort_words(1, 0)
+        quantise_pair(0, 1)
+        spread_biases(bank_sets[0], (GATE_F, GATE_O))
+        transpose_pair(1, 0, bank_sets[0])
+        quantise_pair(1, 0)
+        first_sums = open_banks(bank_sets[0], whole_tiles)
+        run_passes(
+            first_sums, whole_tiles, first_q, first_j, [(k, m) for k in range(GROUPS) for m in tiles]
+        )
+        sort_words(1, 1)
+        transpose_pair(1, 1, bank_sets[0])
+        quantise_pair(1, 1)
+        run_passes(
+            first_sums, whole_tiles, first_q, first_j,
+            [(k, m) for m in tiles for k in range(GROUPS, PASSES)],
+        )
+        first_set = 0
 
         gate = {}
         new_part = {}
         kept_part = {}
         tanh_c = {}
 
-        def form_new_part(j, m):
+        def form_new_part(j, m, first, width):
             new_part[j, m] = work.tile([P, N_TILE], F32, tag="new_part", name="new_part")
             nc.vector.tensor_tensor(
-                out=new_part[j, m][:], in0=gate[GATE_I, j, m][:], in1=gate[GATE_G, j, m][:], op=MULT
+                out=new_part[j, m][:], in0=gate[GATE_I, j, m, 0][:], in1=gate[GATE_G, j, m, 0][:], op=MULT
             )
 
-        def form_kept_part(j, m):
+        def form_kept_part(j, m, first, width):
             kept_part[j, m] = work.tile([P, N_TILE], F32, tag="kept_part", name="kept_part")
             nc.vector.tensor_tensor(
-                out=kept_part[j, m][:], in0=gate[GATE_F, j, m][:], in1=c_half[j][:, m, :], op=MULT
+                out=kept_part[j, m][:], in0=gate[GATE_F, j, m, 0][:], in1=c_half[j][:, m, :], op=MULT
             )
 
-        def finish_cell(j, m):
+        def finish_cell(j, m, first, width):
             c_new = work.tile([P, N_TILE], F32, tag="c_new")
             nc.vector.tensor_tensor(
                 out=c_new[:], in0=kept_part[j, m][:], in1=new_part[j, m][:], op=ADD
@@ -309,14 +337,18 @@ def tile_forcedgpulstmcell_kernel(
             tanh_c[j, m] = work.tile([P, N_TILE], F32, tag="tanh_c", name="tanh_c", bufs=4)
             nc.scalar.activation(out=tanh_c[j, m][:], in_=c_new[:], func=TANH)
 
-        def finish_hidden(j, m):
-            h_new = work.tile([P, N_TILE], F32, tag="h_new", bufs=4)
+        def finish_hidden(j, m, first, width):
+            h_new = work.tile([P, width], F32, tag="h_new", bufs=4)
             engine = nc.gpsimd if False else nc.vector
             engine.tensor_tensor(
-                out=h_new[:], in0=gate[GATE_O, j, m][:], in1=tanh_c[j, m][:], op=MULT
+                out=h_new[:],
+                in0=gate[GATE_O, j, m, first][:],
+                in1=tanh_c[j, m][:, first : first + width],
+                op=MULT,
             )
             nc.sync.dma_start(
-                out=out_0[P * m : P * (m + 1), N_TILE * j : N_TILE * (j + 1)], in_=h_new[:]
+                out=out_0[P * m : P * (m + 1), N_TILE * j + first : N_TILE * j + first + width],
+                in_=h_new[:],
             )
 
         gate_func = {GATE_I: SIGMOID, GATE_G: TANH, GATE_F: SIGMOID, GATE_O: SIGMOID}
@@ -327,30 +359,30 @@ def tile_forcedgpulstmcell_kernel(
             GATE_O: (finish_hidden,),
         }
 
-        banks = len(units) * M_TILES
+        banks = sum([len(pieces) for pieces in unit_pieces])
         later = [[] for b in range(banks + LAG + 2)]
         b = 0
         for u, (q, j) in enumerate(units):
+            pieces = unit_pieces[u]
             if u == 0:
                 sums = first_sums
             else:
-                sums = open_banks(bank_sets[(first_set + u) % 2])
-                if u < 1:
-                    run_passes(sums, q, j, [(k, m) for k in range(PASSES) for m in tiles])
-                else:
-                    run_passes(sums, q, j, [(k, m) for m in tiles for k in range(PASSES)])
-            for m in tiles:
-                value = work.tile([P, N_TILE], F32, tag="gate_%d" % q, name="gate_%d" % q)
+                sums = open_banks(bank_sets[(first_set + u) % 2], pieces)
+                run_passes(
+                    sums, pieces, q, j, [(k, n) for n in range(len(pieces)) for k in range(PASSES)]
+                )
+            for n, (m, first, width) in enumerate(pieces):
+                value = work.tile([P, width], F32, tag="gate_%d" % q, name="gate_%d" % q)
                 nc.vector.tensor_tensor(
-                    out=value[:], in0=sums[m][:], in1=bias_all[:, q, j, :], op=ADD
+                    out=value[:], in0=sums[n][:], in1=bias_all[:, q, j, first : first + width], op=ADD
                 )
                 nc.scalar.activation(out=value[:], in_=value[:], func=gate_func[q])
-                gate[q, j, m] = value
-                for n, step in enumerate(next_steps[q]):
-                    later[b + LAG + n].append((step, j, m))
-                for step, step_j, step_m in later[b]:
-                    step(step_j, step_m)
+                gate[q, j, m, first] = value
+                for wait, step in enumerate(next_steps[q]):
+                    later[b + LAG + wait].append((step, (j, m, first, width)))
+                for step, piece in later[b]:
+                    step(*piece)
                 b += 1
         for steps in later[banks:]:
-            for step, step_j, step_m in steps:
-                step(step_j, step_m)
+            for step, piece in steps:
+                step(*piece)

@@ -51,7 +51,7 @@ def tile_forcedgpulstmcell_kernel(
         ((weight_io_words, weight_ho_words), (weight_io_scales, weight_ho_scales), bias_o),
     )
     GATE_I, GATE_G, GATE_F, GATE_O = 0, 1, 2, 3
-    units = ((GATE_I, 0), (GATE_G, 0), (GATE_F, 0), (GATE_O, 0), (GATE_I, 1), (GATE_G, 1), (GATE_F, 1), (GATE_O, 1))
+    units = ((GATE_I, 0, (0, 1, 2, 3,)), (GATE_G, 0, (0, 1, 2, 3,)), (GATE_F, 0, (0, 1, 2, 3,)), (GATE_O, 0, (0, 1, 2, 3,)), (GATE_I, 1, (0, 1, 2, 3,)), (GATE_G, 1, (0, 1, 2, 3,)), (GATE_F, 1, (0, 1, 2, 3,)), (GATE_O, 1, (0, 1, 2, 3,)))
 
     with ExitStack() as ctx:
         const = ctx.enter_context(tc.tile_pool(name="const", bufs=1))
@@ -68,7 +68,7 @@ def tile_forcedgpulstmcell_kernel(
         for q in range(GATES):
             for s in range(SOURCES):
                 w_planes[q, s] = weights.tile(
-                    [P, HIDDEN], U8, name="w_planes_%d_%d" % (q, s), align_bytes=64
+                    [P, HIDDEN], U8, name="w_planes_%d_%d" % (q, s), align_bytes=256
                 )
                 nc.vector.memset(w_planes[q, s][:].bitcast(I32), 0)
         raw = {}
@@ -103,7 +103,7 @@ def tile_forcedgpulstmcell_kernel(
 
         def load_words(q, s, j):
             w_words[q, s, j] = weights.tile(
-                [P, GROUPS, N_TILE], U32, name="w_words_%d_%d_%d" % (q, s, j), align_bytes=64
+                [P, GROUPS, N_TILE], U32, name="w_words_%d_%d_%d" % (q, s, j), align_bytes=256
             )
             by_bytes = gate_inputs[q][0][s].rearrange("g p n t -> p g (n t)")
             nc.sync.dma_start(
@@ -118,7 +118,11 @@ def tile_forcedgpulstmcell_kernel(
                 in_=c.rearrange("(m p) n -> p m n", p=P)[:, :, N_TILE * j : N_TILE * (j + 1)],
             )
 
-        first_q, first_j = units[0]
+        later_loads = []
+        for q, j, unit_tiles in units[1:]:
+            if (q, j) != units[0][:2] and (q, j) not in later_loads:
+                later_loads.append((q, j))
+        first_q, first_j = units[0][:2]
         load_bias_rows()
         load_pair(0, 0)
         load_pair(0, 1)
@@ -128,7 +132,7 @@ def tile_forcedgpulstmcell_kernel(
         load_pair(1, 1)
         load_scales(first_q, 1)
         load_words(first_q, 1, first_j)
-        for q, j in units[1:]:
+        for q, j in later_loads:
             if q == GATE_F:
                 load_c(j)
             if j == 0:
@@ -149,6 +153,8 @@ def tile_forcedgpulstmcell_kernel(
 
         bias_all = const.tile([P, GATES, N_HALVES, N_TILE], BF16)
 
+        spreads = {}
+
         def spread_biases(bank_set, spread_gates):
             for q in spread_gates:
                 spread = psum.tile([P, N_HALVES, N_TILE], BF16, tag=bank_set, name="spread")
@@ -161,7 +167,11 @@ def tile_forcedgpulstmcell_kernel(
                         start=True,
                         stop=True,
                     )
-                nc.scalar.copy(out=bias_all[:, q, :, :], in_=spread[:])
+                spreads[q] = spread
+
+        def copy_biases(spread_gates):
+            for q in spread_gates:
+                nc.scalar.copy(out=bias_all[:, q, :, :], in_=spreads[q][:])
 
         z_codes = {}
         z_scales = {}
@@ -188,7 +198,7 @@ def tile_forcedgpulstmcell_kernel(
                                 ident_f32[:],
                             )
                     grouped = acts.tile(
-                        [P, 2 * P, PACK], BF16, name="grouped", tag="grouped", bufs=4, align_bytes=64
+                        [P, 2 * P, PACK], BF16, name="grouped", tag="grouped", bufs=4, align_bytes=256
                     )
                     grouped_flat = grouped[:].rearrange("p b t -> p (b t)")
                     grouped_words = grouped_flat.bitcast(F32).rearrange("p (b u) -> p b u", u=2)
@@ -199,10 +209,10 @@ def tile_forcedgpulstmcell_kernel(
                     else:
                         nc.scalar.copy(out=grouped_words, in_=flipped[:].rearrange("p u b -> p b u"))
                     z_codes[k, mp] = acts.tile(
-                        [P, 2 * P], U32, name="z_codes_%d_%d" % (k, mp), align_bytes=64
+                        [P, 2 * P], U32, name="z_codes_%d_%d" % (k, mp), align_bytes=256
                     )
                     z_scales[k, mp] = acts.tile(
-                        [P, 2 * P], U8, name="z_scales_%d_%d" % (k, mp), align_bytes=64
+                        [P, 2 * P], U8, name="z_scales_%d_%d" % (k, mp), align_bytes=256
                     )
                     nc.vector.quantize_mx(
                         out=z_codes[k, mp][:].bitcast(FP8X4),
@@ -239,7 +249,7 @@ def tile_forcedgpulstmcell_kernel(
             grouped_flat = {}
             for g, copy in enumerate((nc.vector.tensor_copy, nc.scalar.copy)):
                 grouped = acts.tile(
-                    [P, 2 * P, PACK], BF16, name="grouped", tag="grouped", bufs=4, align_bytes=64
+                    [P, 2 * P, PACK], BF16, name="grouped", tag="grouped", bufs=4, align_bytes=256
                 )
                 grouped_flat[g] = grouped[:].rearrange("p b t -> p (b t)")
                 copy(
@@ -249,10 +259,10 @@ def tile_forcedgpulstmcell_kernel(
             for g in range(GROUPS):
                 k = GROUPS * s + g
                 z_codes[k, mp] = acts.tile(
-                    [P, 2 * P], U32, name="z_codes_%d_%d" % (k, mp), align_bytes=64
+                    [P, 2 * P], U32, name="z_codes_%d_%d" % (k, mp), align_bytes=256
                 )
                 z_scales[k, mp] = acts.tile(
-                    [P, 2 * P], U8, name="z_scales_%d_%d" % (k, mp), align_bytes=64
+                    [P, 2 * P], U8, name="z_scales_%d_%d" % (k, mp), align_bytes=256
                 )
                 nc.vector.quantize_mx(
                     out=z_codes[k, mp][:].bitcast(FP8X4),
@@ -261,7 +271,7 @@ def tile_forcedgpulstmcell_kernel(
                 )
 
         whole_tiles = [(m, 0, N_TILE) for m in range(M_TILES)]
-        unit_pieces = [whole_tiles for unit in units]
+        unit_pieces = [[(m, 0, N_TILE) for m in unit_tiles] for q, j, unit_tiles in units]
 
         def open_banks(bank_set, pieces):
             return [
@@ -287,6 +297,7 @@ def tile_forcedgpulstmcell_kernel(
         tiles = range(M_TILES)
         sort_words(0, 0)
         spread_biases(bank_sets[0], (GATE_I, GATE_G))
+        copy_biases((GATE_I, GATE_G))
         transpose_pair(0, 0, bank_sets[0])
         sort_words(0, 1)
         quantise_pair(0, 0)
@@ -294,6 +305,7 @@ def tile_forcedgpulstmcell_kernel(
         sort_words(1, 0)
         quantise_pair(0, 1)
         spread_biases(bank_sets[0], (GATE_F, GATE_O))
+        copy_biases((GATE_F, GATE_O))
         transpose_pair(1, 0, bank_sets[0])
         quantise_pair(1, 0)
         first_sums = open_banks(bank_sets[0], whole_tiles)
@@ -362,7 +374,7 @@ def tile_forcedgpulstmcell_kernel(
         banks = sum([len(pieces) for pieces in unit_pieces])
         later = [[] for b in range(banks + LAG + 2)]
         b = 0
-        for u, (q, j) in enumerate(units):
+        for u, (q, j, unit_tiles) in enumerate(units):
             pieces = unit_pieces[u]
             if u == 0:
                 sums = first_sums

@@ -62,7 +62,7 @@ def tile_forcedgpulstmcell_kernel(
         bank_sets = ("bank", "bank")
         ctx.enter_context(tc.manual_schedule())
 
-        bias_rows = const.tile([P, N_TILE], BF16)
+        bias_rows = const.tile([P, N_TILE], BF16, align_bytes=256)
         nc.vector.memset(bias_rows[:], 0.0)
         w_planes = {}
         for q in range(GATES):
@@ -84,7 +84,7 @@ def tile_forcedgpulstmcell_kernel(
 
         def load_pair(s, mp):
             by_pair = (x, h)[s].rearrange("(mp m p) k -> mp p m k", m=2, p=P)
-            raw[s, mp] = acts.tile([P, 2, FEATURES], BF16, name="raw_%d_%d" % (s, mp))
+            raw[s, mp] = acts.tile([P, 2, FEATURES], BF16, name="raw_%d_%d" % (s, mp), align_bytes=256)
             nc.sync.dma_start(out=raw[s, mp][:], in_=by_pair[mp])
 
         def load_source(s):
@@ -112,7 +112,7 @@ def tile_forcedgpulstmcell_kernel(
             )
 
         def load_c(j):
-            c_half[j] = acts.tile([P, M_TILES, N_TILE], BF16, name="c_half_%d" % j)
+            c_half[j] = acts.tile([P, M_TILES, N_TILE], BF16, name="c_half_%d" % j, align_bytes=256)
             nc.sync.dma_start(
                 out=c_half[j][:],
                 in_=c.rearrange("(m p) n -> p m n", p=P)[:, :, N_TILE * j : N_TILE * (j + 1)],
@@ -339,7 +339,7 @@ def tile_forcedgpulstmcell_kernel(
             )
 
         def finish_cell(j, m, first, width):
-            c_new = work.tile([P, N_TILE], F32, tag="c_new")
+            c_new = work.tile([P, N_TILE], F32, tag="c_new", align_bytes=256)
             nc.vector.tensor_tensor(
                 out=c_new[:], in0=kept_part[j, m][:], in1=new_part[j, m][:], op=ADD
             )
@@ -350,7 +350,7 @@ def tile_forcedgpulstmcell_kernel(
             nc.scalar.activation(out=tanh_c[j, m][:], in_=c_new[:], func=TANH)
 
         def finish_hidden(j, m, first, width):
-            h_new = work.tile([P, width], F32, tag="h_new", bufs=4)
+            h_new = work.tile([P, width], F32, tag="h_new", bufs=4, align_bytes=256)
             engine = nc.gpsimd if False else nc.vector
             engine.tensor_tensor(
                 out=h_new[:],

@@ -28,6 +28,7 @@ N_HALVES = HIDDEN // N_TILE
 GATES = 4
 LAG = 2
 SORT_AHEAD = 1
+SPLIT_TILES = 2
 PLANE_ROWS = 4
 
 FLOPS = 2 * BATCH * (SOURCES * FEATURES) * (GATES * HIDDEN)
@@ -51,7 +52,7 @@ def tile_forcedgpulstmcell_kernel(
         ((weight_io_words, weight_ho_words), (weight_io_scales, weight_ho_scales), bias_o),
     )
     GATE_I, GATE_G, GATE_F, GATE_O = 0, 1, 2, 3
-    units = ((GATE_I, 0, (0, 1, 2, 3,)), (GATE_G, 0, (0, 1, 2, 3,)), (GATE_F, 0, (0, 1, 2, 3,)), (GATE_O, 0, (0, 1, 2, 3,)), (GATE_I, 1, (0, 1, 2, 3,)), (GATE_G, 1, (0, 1, 2, 3,)), (GATE_F, 1, (0, 1, 2, 3,)), (GATE_O, 1, (0, 1, 2, 3,)))
+    units = ((GATE_I, 0, (0, 1, 2, 3,)), (GATE_G, 0, (0, 1, 2, 3,)), (GATE_F, 0, (0, 1, 2, 3,)), (GATE_I, 1, (0, 1, 2, 3,)), (GATE_G, 1, (0, 1, 2, 3,)), (GATE_F, 1, (0, 1, 2, 3,)), (GATE_O, 0, (0, 1, 2, 3,)), (GATE_O, 1, (0, 1, 2, 3,)))
 
     with ExitStack() as ctx:
         const = ctx.enter_context(tc.tile_pool(name="const", bufs=1))
@@ -76,7 +77,7 @@ def tile_forcedgpulstmcell_kernel(
         c_half = {}
 
         def load_bias_rows():
-            for q in range(GATES):
+            for q in (GATE_I, GATE_G, GATE_F):
                 nc.sync.dma_start(
                     out=bias_rows[N_HALVES * q : N_HALVES * (q + 1), :],
                     in_=gate_inputs[q][2].rearrange("(j n) -> j n", j=N_HALVES),
@@ -133,14 +134,14 @@ def tile_forcedgpulstmcell_kernel(
         load_scales(first_q, 1)
         load_words(first_q, 1, first_j)
         for q, j in later_loads:
-            if q == GATE_F:
-                load_c(j)
             if j == 0:
                 load_scales(q, 0)
             load_words(q, 0, j)
             load_words(q, 1, j)
             if j == 0:
                 load_scales(q, 1)
+            if q == GATE_F:
+                load_c(j)
 
         warm = const.tile([P, 1], F32)
         nc.vector.memset(warm[:], 0.0)
@@ -151,7 +152,11 @@ def tile_forcedgpulstmcell_kernel(
         make_identity(nc, ident_bf16[:])
         make_identity(nc, ident_f32[:])
 
-        bias_all = const.tile([P, GATES, N_HALVES, N_TILE], BF16)
+        bias_all = const.tile([P, GATES, N_HALVES, N_TILE], BF16, align_bytes=256)
+        nc.sync.dma_start(
+            out=bias_all[:, GATE_O, :, :].rearrange("p j n -> p (j n)"),
+            in_=bias_o.partition_broadcast(P),
+        )
 
         spreads = {}
 
@@ -272,6 +277,11 @@ def tile_forcedgpulstmcell_kernel(
 
         whole_tiles = [(m, 0, N_TILE) for m in range(M_TILES)]
         unit_pieces = [[(m, 0, N_TILE) for m in unit_tiles] for q, j, unit_tiles in units]
+        unit_pieces[-1] = unit_pieces[-1][:-SPLIT_TILES] + [
+            (m, first, N_TILE // 2)
+            for m in range(M_TILES - SPLIT_TILES, M_TILES)
+            for first in (0, N_TILE // 2)
+        ]
 
         def open_banks(bank_set, pieces):
             return [
@@ -304,8 +314,8 @@ def tile_forcedgpulstmcell_kernel(
         transpose_pair(0, 1, bank_sets[0])
         sort_words(1, 0)
         quantise_pair(0, 1)
-        spread_biases(bank_sets[0], (GATE_F, GATE_O))
-        copy_biases((GATE_F, GATE_O))
+        spread_biases(bank_sets[0], (GATE_F,))
+        copy_biases((GATE_F,))
         transpose_pair(1, 0, bank_sets[0])
         quantise_pair(1, 0)
         first_sums = open_banks(bank_sets[0], whole_tiles)
@@ -346,11 +356,11 @@ def tile_forcedgpulstmcell_kernel(
             nc.sync.dma_start(
                 out=out_1[P * m : P * (m + 1), N_TILE * j : N_TILE * (j + 1)], in_=c_new[:]
             )
-            tanh_c[j, m] = work.tile([P, N_TILE], F32, tag="tanh_c", name="tanh_c", bufs=4)
+            tanh_c[j, m] = work.tile([P, N_TILE], F32, tag="tanh_c", name="tanh_c", bufs=8)
             nc.scalar.activation(out=tanh_c[j, m][:], in_=c_new[:], func=TANH)
 
         def finish_hidden(j, m, first, width):
-            h_new = work.tile([P, width], F32, tag="h_new", bufs=4, align_bytes=256)
+            h_new = work.tile([P, width], F32, tag="h_new", bufs=8, align_bytes=256)
             engine = nc.gpsimd if False else nc.vector
             engine.tensor_tensor(
                 out=h_new[:],

@@ -26,9 +26,8 @@ M_PAIRS = M_TILES // 2
 N_TILE = 512
 N_HALVES = HIDDEN // N_TILE
 GATES = 4
-LAG = 2
 SORT_AHEAD = 1
-SPLIT_TILES = 2
+HALF = N_TILE // 2
 PLANE_ROWS = 4
 
 FLOPS = 2 * BATCH * (SOURCES * FEATURES) * (GATES * HIDDEN)
@@ -52,7 +51,7 @@ def tile_forcedgpulstmcell_kernel(
         ((weight_io_words, weight_ho_words), (weight_io_scales, weight_ho_scales), bias_o),
     )
     GATE_I, GATE_G, GATE_F, GATE_O = 0, 1, 2, 3
-    units = ((GATE_I, 0, (0, 1, 2, 3,)), (GATE_G, 0, (0, 1, 2, 3,)), (GATE_F, 0, (0, 1, 2, 3,)), (GATE_I, 1, (0, 1, 2, 3,)), (GATE_G, 1, (0, 1, 2, 3,)), (GATE_F, 1, (0, 1, 2, 3,)), (GATE_O, 0, (0, 1, 2, 3,)), (GATE_O, 1, (0, 1, 2, 3,)))
+    tiles = range(M_TILES)
 
     with ExitStack() as ctx:
         const = ctx.enter_context(tc.tile_pool(name="const", bufs=1))
@@ -60,7 +59,6 @@ def tile_forcedgpulstmcell_kernel(
         weights = ctx.enter_context(tc.tile_pool(name="weights", bufs=1))
         work = ctx.enter_context(tc.tile_pool(name="work", bufs=M_TILES))
         psum = ctx.enter_context(tc.psum_pool(name="psum", bufs=2 * M_TILES))
-        bank_sets = ("bank", "bank")
         ctx.enter_context(tc.manual_schedule())
 
         bias_rows = const.tile([P, N_TILE], BF16, align_bytes=256)
@@ -102,15 +100,17 @@ def tile_forcedgpulstmcell_kernel(
                     ].bitcast(I32),
                 )
 
-        def load_words(q, s, j):
-            w_words[q, s, j] = weights.tile(
-                [P, GROUPS, N_TILE], U32, name="w_words_%d_%d_%d" % (q, s, j), align_bytes=256
+        def load_words(q, s, j, halves=1):
+            words = weights.tile(
+                [P, GROUPS, halves * N_TILE], U32, name="w_words_%d_%d_%d" % (q, s, j), align_bytes=256
             )
             by_bytes = gate_inputs[q][0][s].rearrange("g p n t -> p g (n t)")
             nc.sync.dma_start(
-                out=w_words[q, s, j][:].bitcast(I32),
-                in_=by_bytes[:, :, PACK * N_TILE * j : PACK * N_TILE * (j + 1)].bitcast(I32),
+                out=words[:].bitcast(I32),
+                in_=by_bytes[:, :, PACK * N_TILE * j : PACK * N_TILE * (j + halves)].bitcast(I32),
             )
+            for half in range(j, j + halves):
+                w_words[q, s, half] = (words, N_TILE * (half - j))
 
         def load_c(j):
             c_half[j] = acts.tile([P, M_TILES, N_TILE], BF16, name="c_half_%d" % j, align_bytes=256)
@@ -119,29 +119,47 @@ def tile_forcedgpulstmcell_kernel(
                 in_=c.rearrange("(m p) n -> p m n", p=P)[:, :, N_TILE * j : N_TILE * (j + 1)],
             )
 
-        later_loads = []
-        for q, j, unit_tiles in units[1:]:
-            if (q, j) != units[0][:2] and (q, j) not in later_loads:
-                later_loads.append((q, j))
-        first_q, first_j = units[0][:2]
+        bias_all = const.tile([P, GATES, N_HALVES, N_TILE], BF16, align_bytes=256)
+
+        def load_bias_o():
+            nc.sync.dma_start(
+                out=bias_all[:, GATE_O, :, :].rearrange("p j n -> p (j n)"),
+                in_=bias_o.partition_broadcast(P),
+            )
+
+        first_q, first_j = GATE_I, 0
         load_bias_rows()
         load_pair(0, 0)
         load_pair(0, 1)
         load_pair(1, 0)
-        load_scales(first_q, 0)
-        load_words(first_q, 0, first_j)
+        load_scales(GATE_I, 0)
+        load_words(GATE_I, 0, 0)
         load_pair(1, 1)
-        load_scales(first_q, 1)
-        load_words(first_q, 1, first_j)
-        for q, j in later_loads:
-            if j == 0:
-                load_scales(q, 0)
-            load_words(q, 0, j)
-            load_words(q, 1, j)
-            if j == 0:
-                load_scales(q, 1)
-            if q == GATE_F:
-                load_c(j)
+        load_scales(GATE_I, 1)
+        load_words(GATE_I, 1, 0)
+        load_scales(GATE_G, 0)
+        load_words(GATE_G, 0, 0)
+        load_words(GATE_G, 1, 0)
+        load_scales(GATE_G, 1)
+        load_scales(GATE_F, 0)
+        load_words(GATE_F, 0, 0)
+        load_words(GATE_F, 1, 0)
+        load_scales(GATE_F, 1)
+        load_words(GATE_I, 0, 1)
+        load_c(0)
+        load_words(GATE_I, 1, 1)
+        load_words(GATE_G, 0, 1)
+        load_words(GATE_G, 1, 1)
+        load_words(GATE_F, 0, 1)
+        load_words(GATE_F, 1, 1)
+        load_scales(GATE_O, 0)
+        load_words(GATE_O, 0, 0)
+        load_words(GATE_O, 1, 0)
+        load_scales(GATE_O, 1)
+        load_bias_o()
+        load_c(1)
+        load_words(GATE_O, 0, 1)
+        load_words(GATE_O, 1, 1)
 
         warm = const.tile([P, 1], F32)
         nc.vector.memset(warm[:], 0.0)
@@ -151,12 +169,6 @@ def tile_forcedgpulstmcell_kernel(
         ident_f32 = const.tile([P, P], F32)
         make_identity(nc, ident_bf16[:])
         make_identity(nc, ident_f32[:])
-
-        bias_all = const.tile([P, GATES, N_HALVES, N_TILE], BF16, align_bytes=256)
-        nc.sync.dma_start(
-            out=bias_all[:, GATE_O, :, :].rearrange("p j n -> p (j n)"),
-            in_=bias_o.partition_broadcast(P),
-        )
 
         spreads = {}
 
@@ -180,50 +192,6 @@ def tile_forcedgpulstmcell_kernel(
 
         z_codes = {}
         z_scales = {}
-
-        def quantise_source(s, bank_set, pairs):
-            for mp in pairs:
-                words = raw[s, mp][:].bitcast(F32)
-                sorted_words = acts.tile(
-                    [P, 2, GROUPS, 2, P], F32, name="sorted_words", tag="sorted_words", bufs=2
-                )
-                for m, copy in enumerate((nc.vector.tensor_copy, nc.scalar.copy)):
-                    copy(
-                        out=sorted_words[:, m, :, :, :],
-                        in_=words[:, m, :].rearrange("p (g w u) -> p g u w", g=GROUPS, u=2),
-                    )
-                for g in range(GROUPS):
-                    k = GROUPS * s + g
-                    flipped = psum.tile([P, 2, 2 * P], F32, tag=bank_set, name="flipped")
-                    for u in range(2):
-                        for m in range(2):
-                            nc.tensor.transpose(
-                                flipped[:, u, P * m : P * (m + 1)],
-                                sorted_words[:, m, g, u, :],
-                                ident_f32[:],
-                            )
-                    grouped = acts.tile(
-                        [P, 2 * P, PACK], BF16, name="grouped", tag="grouped", bufs=4, align_bytes=256
-                    )
-                    grouped_flat = grouped[:].rearrange("p b t -> p (b t)")
-                    grouped_words = grouped_flat.bitcast(F32).rearrange("p (b u) -> p b u", u=2)
-                    if g % 2 == 0:
-                        nc.vector.tensor_copy(
-                            out=grouped_words, in_=flipped[:].rearrange("p u b -> p b u")
-                        )
-                    else:
-                        nc.scalar.copy(out=grouped_words, in_=flipped[:].rearrange("p u b -> p b u"))
-                    z_codes[k, mp] = acts.tile(
-                        [P, 2 * P], U32, name="z_codes_%d_%d" % (k, mp), align_bytes=256
-                    )
-                    z_scales[k, mp] = acts.tile(
-                        [P, 2 * P], U8, name="z_scales_%d_%d" % (k, mp), align_bytes=256
-                    )
-                    nc.vector.quantize_mx(
-                        out=z_codes[k, mp][:].bitcast(FP8X4),
-                        scales=z_scales[k, mp][:],
-                        in_=grouped_flat,
-                    )
 
         sorted_words = {}
         flipped_banks = {}
@@ -275,94 +243,84 @@ def tile_forcedgpulstmcell_kernel(
                     in_=grouped_flat[g],
                 )
 
-        whole_tiles = [(m, 0, N_TILE) for m in range(M_TILES)]
-        unit_pieces = [[(m, 0, N_TILE) for m in unit_tiles] for q, j, unit_tiles in units]
-        unit_pieces[-1] = unit_pieces[-1][:-SPLIT_TILES] + [
-            (m, first, N_TILE // 2)
-            for m in range(M_TILES - SPLIT_TILES, M_TILES)
-            for first in (0, N_TILE // 2)
-        ]
+        def open_bank(m, first, width):
+            return psum.tile([P, width], F32, tag="bank", name="sums_%d_%d" % (m, first))
 
-        def open_banks(bank_set, pieces):
-            return [
-                psum.tile([P, width], F32, tag=bank_set, name="sums_%d_%d" % (m, first))
-                for m, first, width in pieces
-            ]
+        def run_pass(sums, q, j, m, first, width, k):
+            rows = slice(P * (m % 2), P * (m % 2 + 1))
+            columns = slice(N_TILE * j + first, N_TILE * j + first + width)
+            words, begin = w_words[q, k // GROUPS, j]
+            nc.tensor.matmul_mx(
+                out=sums[:],
+                lhsT=z_codes[k, m // 2][:, rows].bitcast(FP8X4),
+                lhsT_scale=z_scales[k, m // 2][:, rows],
+                rhs=words[:, k % GROUPS, begin + first : begin + first + width].bitcast(FP8X4),
+                rhs_scale=w_planes[q, k // GROUPS][PLANE_ROWS * (k % GROUPS) : P, columns],
+                start=(k == 0),
+                stop=(k == PASSES - 1),
+            )
 
-        def run_passes(sums, pieces, q, j, pass_order):
-            for k, n in pass_order:
-                m, first, width = pieces[n]
-                rows = slice(P * (m % 2), P * (m % 2 + 1))
-                columns = slice(N_TILE * j + first, N_TILE * j + first + width)
-                nc.tensor.matmul_mx(
-                    out=sums[n][:],
-                    lhsT=z_codes[k, m // 2][:, rows].bitcast(FP8X4),
-                    lhsT_scale=z_scales[k, m // 2][:, rows],
-                    rhs=w_words[q, k // GROUPS, j][:, k % GROUPS, first : first + width].bitcast(FP8X4),
-                    rhs_scale=w_planes[q, k // GROUPS][PLANE_ROWS * (k % GROUPS) : P, columns],
-                    start=(k == 0),
-                    stop=(k == PASSES - 1),
-                )
-
-        tiles = range(M_TILES)
         sort_words(0, 0)
-        spread_biases(bank_sets[0], (GATE_I, GATE_G))
+        spread_biases("bank", (GATE_I, GATE_G))
         copy_biases((GATE_I, GATE_G))
-        transpose_pair(0, 0, bank_sets[0])
+        transpose_pair(0, 0, "bank")
         sort_words(0, 1)
         quantise_pair(0, 0)
-        transpose_pair(0, 1, bank_sets[0])
+        transpose_pair(0, 1, "bank")
         sort_words(1, 0)
         quantise_pair(0, 1)
-        spread_biases(bank_sets[0], (GATE_F,))
+        spread_biases("bank", (GATE_F,))
         copy_biases((GATE_F,))
-        transpose_pair(1, 0, bank_sets[0])
+        transpose_pair(1, 0, "bank")
         quantise_pair(1, 0)
-        first_sums = open_banks(bank_sets[0], whole_tiles)
-        run_passes(
-            first_sums, whole_tiles, first_q, first_j, [(k, m) for k in range(GROUPS) for m in tiles]
-        )
+        first_sums = []
+        for m in tiles:
+            sums = open_bank(m, 0, N_TILE)
+            first_sums.append(sums)
+        for k in range(GROUPS):
+            for m in tiles:
+                run_pass(first_sums[m], first_q, first_j, m, 0, N_TILE, k)
         sort_words(1, 1)
-        transpose_pair(1, 1, bank_sets[0])
+        transpose_pair(1, 1, "bank")
         quantise_pair(1, 1)
-        run_passes(
-            first_sums, whole_tiles, first_q, first_j,
-            [(k, m) for m in tiles for k in range(GROUPS, PASSES)],
-        )
-        first_set = 0
+        for m in tiles:
+            for k in range(GROUPS, PASSES):
+                run_pass(first_sums[m], first_q, first_j, m, 0, N_TILE, k)
 
         gate = {}
         new_part = {}
         kept_part = {}
+        cell = {}
         tanh_c = {}
 
-        def form_new_part(j, m, first, width):
+        def form_new_part(j, m):
             new_part[j, m] = work.tile([P, N_TILE], F32, tag="new_part", name="new_part")
-            nc.vector.tensor_tensor(
+            (nc.gpsimd if (j, m) in ((1, 0), (1, 1), (1, 2), (1, 3)) else nc.vector).tensor_tensor(
                 out=new_part[j, m][:], in0=gate[GATE_I, j, m, 0][:], in1=gate[GATE_G, j, m, 0][:], op=MULT
             )
 
-        def form_kept_part(j, m, first, width):
+        def form_kept_part(j, m):
             kept_part[j, m] = work.tile([P, N_TILE], F32, tag="kept_part", name="kept_part")
             nc.vector.tensor_tensor(
                 out=kept_part[j, m][:], in0=gate[GATE_F, j, m, 0][:], in1=c_half[j][:, m, :], op=MULT
             )
 
-        def finish_cell(j, m, first, width):
-            c_new = work.tile([P, N_TILE], F32, tag="c_new", align_bytes=256)
-            nc.vector.tensor_tensor(
-                out=c_new[:], in0=kept_part[j, m][:], in1=new_part[j, m][:], op=ADD
+        def form_cell(j, m):
+            cell[j, m] = work.tile([P, N_TILE], F32, tag="c_new", name="c_new", bufs=8, align_bytes=256)
+            (nc.gpsimd if (j, m) in ((1, 0), (1, 1), (1, 2), (1, 3)) else nc.vector).tensor_tensor(
+                out=cell[j, m][:], in0=kept_part[j, m][:], in1=new_part[j, m][:], op=ADD
             )
             nc.sync.dma_start(
-                out=out_1[P * m : P * (m + 1), N_TILE * j : N_TILE * (j + 1)], in_=c_new[:]
+                out=out_1[P * m : P * (m + 1), N_TILE * j : N_TILE * (j + 1)], in_=cell[j, m][:]
             )
-            tanh_c[j, m] = work.tile([P, N_TILE], F32, tag="tanh_c", name="tanh_c", bufs=8)
-            nc.scalar.activation(out=tanh_c[j, m][:], in_=c_new[:], func=TANH)
 
-        def finish_hidden(j, m, first, width):
+        def form_tanh(j, m):
+            tanh_c[j, m] = work.tile([P, N_TILE], F32, tag="tanh_c", name="tanh_c", bufs=8)
+            nc.scalar.activation(out=tanh_c[j, m][:], in_=cell[j, m][:], func=TANH)
+
+        def finish_hidden(j, m, first=0, width=N_TILE):
             h_new = work.tile([P, width], F32, tag="h_new", bufs=8, align_bytes=256)
-            engine = nc.gpsimd if False else nc.vector
-            engine.tensor_tensor(
+            nc.vector.tensor_tensor(
                 out=h_new[:],
                 in0=gate[GATE_O, j, m, first][:],
                 in1=tanh_c[j, m][:, first : first + width],
@@ -374,37 +332,66 @@ def tile_forcedgpulstmcell_kernel(
             )
 
         gate_func = {GATE_I: SIGMOID, GATE_G: TANH, GATE_F: SIGMOID, GATE_O: SIGMOID}
-        next_steps = {
-            GATE_I: (),
-            GATE_G: (form_new_part,),
-            GATE_F: (form_kept_part, finish_cell),
-            GATE_O: (finish_hidden,),
-        }
-
-        banks = sum([len(pieces) for pieces in unit_pieces])
-        later = [[] for b in range(banks + LAG + 2)]
-        b = 0
-        for u, (q, j, unit_tiles) in enumerate(units):
-            pieces = unit_pieces[u]
-            if u == 0:
-                sums = first_sums
+        def use_bank(q, j, m, first=0, width=N_TILE):
+            if (q, j) == (first_q, first_j):
+                sums = first_sums[m]
             else:
-                sums = open_banks(bank_sets[(first_set + u) % 2], pieces)
-                run_passes(
-                    sums, pieces, q, j, [(k, n) for n in range(len(pieces)) for k in range(PASSES)]
-                )
-            for n, (m, first, width) in enumerate(pieces):
-                value = work.tile([P, width], F32, tag="gate_%d" % q, name="gate_%d" % q)
-                nc.vector.tensor_tensor(
-                    out=value[:], in0=sums[n][:], in1=bias_all[:, q, j, first : first + width], op=ADD
-                )
-                nc.scalar.activation(out=value[:], in_=value[:], func=gate_func[q])
-                gate[q, j, m, first] = value
-                for wait, step in enumerate(next_steps[q]):
-                    later[b + LAG + wait].append((step, (j, m, first, width)))
-                for step, piece in later[b]:
-                    step(*piece)
-                b += 1
-        for steps in later[banks:]:
-            for step, piece in steps:
-                step(*piece)
+                sums = open_bank(m, first, width)
+                for k in range(PASSES):
+                    run_pass(sums, q, j, m, first, width, k)
+            value = work.tile([P, width], F32, tag="gate_%d" % q, name="gate_%d" % q)
+            nc.vector.tensor_tensor(
+                out=value[:], in0=sums[:], in1=bias_all[:, q, j, first : first + width], op=ADD
+            )
+            nc.scalar.activation(out=value[:], in_=value[:], func=gate_func[q])
+            gate[q, j, m, first] = value
+
+        for m in tiles:
+            use_bank(GATE_I, 0, m)
+        for m in tiles:
+            use_bank(GATE_G, 0, m)
+            if m >= 2:
+                form_new_part(0, m - 2)
+        for m in tiles:
+            use_bank(GATE_F, 0, m)
+            if m < 2:
+                form_new_part(0, m + 2)
+            else:
+                form_kept_part(0, m - 2)
+        for m in tiles:
+            use_bank(GATE_I, 1, m)
+            if m < 2:
+                form_kept_part(0, m + 2)
+            form_cell(0, m)
+            if m > 0:
+                form_tanh(0, m - 1)
+        for m in tiles:
+            use_bank(GATE_G, 1, m)
+            if m == 0:
+                form_tanh(0, 3)
+            form_new_part(1, m)
+        for m in tiles:
+            use_bank(GATE_F, 1, m)
+            if m < 2:
+                use_bank(GATE_O, 0, m)
+            if m == 2:
+                use_bank(GATE_O, 1, 0)
+            if m == 3:
+                use_bank(GATE_O, 0, 2)
+            if m > 0:
+                form_tanh(1, m - 1)
+                finish_hidden(*((0, 0), (0, 1), (1, 0))[m - 1])
+            form_kept_part(1, m)
+            form_cell(1, m)
+        use_bank(GATE_O, 1, 1)
+        use_bank(GATE_O, 0, 3)
+        form_tanh(1, 3)
+        finish_hidden(0, 2)
+        finish_hidden(1, 1)
+        use_bank(GATE_O, 1, 2)
+        use_bank(GATE_O, 1, 3, 0, HALF)
+        finish_hidden(0, 3)
+        use_bank(GATE_O, 1, 3, HALF, HALF)
+        finish_hidden(1, 2)
+        finish_hidden(1, 3, 0, HALF)
+        finish_hidden(1, 3, HALF, HALF)

@@ -75,7 +75,7 @@ def tile_forcedgpulstmcell_kernel(
         c_half = {}
 
         def load_bias_rows():
-            for q in (GATE_I, GATE_G, GATE_F):
+            for q in (GATE_I, GATE_G, GATE_F, GATE_O):
                 nc.sync.dma_start(
                     out=bias_rows[N_HALVES * q : N_HALVES * (q + 1), :],
                     in_=gate_inputs[q][2].rearrange("(j n) -> j n", j=N_HALVES),
@@ -121,12 +121,6 @@ def tile_forcedgpulstmcell_kernel(
 
         bias_all = const.tile([P, GATES, N_HALVES, N_TILE], BF16, align_bytes=256)
 
-        def load_bias_o():
-            nc.sync.dma_start(
-                out=bias_all[:, GATE_O, :, :].rearrange("p j n -> p (j n)"),
-                in_=bias_o.partition_broadcast(P),
-            )
-
         first_q, first_j = GATE_I, 0
         load_bias_rows()
         load_pair(0, 0)
@@ -145,19 +139,18 @@ def tile_forcedgpulstmcell_kernel(
         load_words(GATE_F, 0, 0)
         load_words(GATE_F, 1, 0)
         load_scales(GATE_F, 1)
-        load_words(GATE_I, 0, 1)
         load_c(0)
+        load_words(GATE_I, 0, 1)
         load_words(GATE_I, 1, 1)
         load_words(GATE_G, 0, 1)
         load_words(GATE_G, 1, 1)
         load_words(GATE_F, 0, 1)
         load_words(GATE_F, 1, 1)
+        load_c(1)
         load_scales(GATE_O, 0)
         load_words(GATE_O, 0, 0)
         load_words(GATE_O, 1, 0)
         load_scales(GATE_O, 1)
-        load_bias_o()
-        load_c(1)
         load_words(GATE_O, 0, 1)
         load_words(GATE_O, 1, 1)
 
@@ -269,8 +262,8 @@ def tile_forcedgpulstmcell_kernel(
         transpose_pair(0, 1, "bank")
         sort_words(1, 0)
         quantise_pair(0, 1)
-        spread_biases("bank", (GATE_F,))
-        copy_biases((GATE_F,))
+        spread_biases("bank", (GATE_F, GATE_O))
+        copy_biases((GATE_F, GATE_O))
         transpose_pair(1, 0, "bank")
         quantise_pair(1, 0)
         first_sums = []
@@ -295,7 +288,7 @@ def tile_forcedgpulstmcell_kernel(
 
         def form_new_part(j, m):
             new_part[j, m] = work.tile([P, N_TILE], F32, tag="new_part", name="new_part")
-            (nc.gpsimd if (j, m) in ((1, 0), (1, 1), (1, 2), (1, 3)) else nc.vector).tensor_tensor(
+            nc.vector.tensor_tensor(
                 out=new_part[j, m][:], in0=gate[GATE_I, j, m, 0][:], in1=gate[GATE_G, j, m, 0][:], op=MULT
             )
 
@@ -307,7 +300,7 @@ def tile_forcedgpulstmcell_kernel(
 
         def form_cell(j, m):
             cell[j, m] = work.tile([P, N_TILE], F32, tag="c_new", name="c_new", bufs=8, align_bytes=256)
-            (nc.gpsimd if (j, m) in ((1, 0), (1, 1), (1, 2), (1, 3)) else nc.vector).tensor_tensor(
+            nc.vector.tensor_tensor(
                 out=cell[j, m][:], in0=kept_part[j, m][:], in1=new_part[j, m][:], op=ADD
             )
             nc.sync.dma_start(
@@ -331,6 +324,15 @@ def tile_forcedgpulstmcell_kernel(
                 in_=h_new[:],
             )
 
+        def finish_hidden_beside(m):
+            h_new = work.tile(
+                [P, N_TILE], F32, tag="gate_%d" % GATE_F, name="gate_%d" % GATE_F, align_bytes=256
+            )
+            nc.gpsimd.tensor_tensor(
+                out=h_new[:], in0=gate[GATE_O, 0, m, 0][:], in1=tanh_c[0, m][:], op=MULT
+            )
+            nc.sync.dma_start(out=out_0[P * m : P * (m + 1), 0:N_TILE], in_=h_new[:])
+
         gate_func = {GATE_I: SIGMOID, GATE_G: TANH, GATE_F: SIGMOID, GATE_O: SIGMOID}
         def use_bank(q, j, m, first=0, width=N_TILE):
             if (q, j) == (first_q, first_j):
@@ -339,7 +341,7 @@ def tile_forcedgpulstmcell_kernel(
                 sums = open_bank(m, first, width)
                 for k in range(PASSES):
                     run_pass(sums, q, j, m, first, width, k)
-            value = work.tile([P, width], F32, tag="gate_%d" % q, name="gate_%d" % q)
+            value = work.tile([P, width], F32, tag="gate_%d" % q, name="gate_%d" % q, align_bytes=256)
             nc.vector.tensor_tensor(
                 out=value[:], in0=sums[:], in1=bias_all[:, q, j, first : first + width], op=ADD
             )
@@ -350,18 +352,18 @@ def tile_forcedgpulstmcell_kernel(
             use_bank(GATE_I, 0, m)
         for m in tiles:
             use_bank(GATE_G, 0, m)
-            if m >= 2:
-                form_new_part(0, m - 2)
+            if m >= 1:
+                form_new_part(0, m - 1)
         for m in tiles:
             use_bank(GATE_F, 0, m)
-            if m < 2:
-                form_new_part(0, m + 2)
+            if m == 0:
+                form_new_part(0, 3)
             else:
-                form_kept_part(0, m - 2)
+                form_kept_part(0, m - 1)
         for m in tiles:
             use_bank(GATE_I, 1, m)
-            if m < 2:
-                form_kept_part(0, m + 2)
+            if m == 0:
+                form_kept_part(0, 3)
             form_cell(0, m)
             if m > 0:
                 form_tanh(0, m - 1)
@@ -369,28 +371,26 @@ def tile_forcedgpulstmcell_kernel(
             use_bank(GATE_G, 1, m)
             if m == 0:
                 form_tanh(0, 3)
-            form_new_part(1, m)
+            else:
+                form_new_part(1, m - 1)
         for m in tiles:
             use_bank(GATE_F, 1, m)
-            if m < 2:
-                use_bank(GATE_O, 0, m)
-            if m == 2:
-                use_bank(GATE_O, 1, 0)
-            if m == 3:
-                use_bank(GATE_O, 0, 2)
-            if m > 0:
+            use_bank(GATE_O, 0, m)
+            if m == 0:
+                form_new_part(1, 3)
+            else:
+                form_cell(1, m - 1)
                 form_tanh(1, m - 1)
-                finish_hidden(*((0, 0), (0, 1), (1, 0))[m - 1])
             form_kept_part(1, m)
-            form_cell(1, m)
+            finish_hidden_beside(m)
+        use_bank(GATE_O, 1, 0)
         use_bank(GATE_O, 1, 1)
-        use_bank(GATE_O, 0, 3)
+        form_cell(1, 3)
         form_tanh(1, 3)
-        finish_hidden(0, 2)
-        finish_hidden(1, 1)
+        finish_hidden(1, 0)
         use_bank(GATE_O, 1, 2)
+        finish_hidden(1, 1)
         use_bank(GATE_O, 1, 3, 0, HALF)
-        finish_hidden(0, 3)
         use_bank(GATE_O, 1, 3, HALF, HALF)
         finish_hidden(1, 2)
         finish_hidden(1, 3, 0, HALF)

@@ -199,29 +199,35 @@ def tile_forcedgpulstmcell_kernel(
                 in_=words.rearrange("p m (g w u) -> p (m g) u w", g=GROUPS, u=2),
             )
 
-        def transpose_pair(s, mp, bank_set):
+        def transpose_pair(s, mp, bank_set, in_place=False):
+            words = raw[s, mp][:].bitcast(F32)
             for g in range(GROUPS):
                 flipped = psum.tile([P, 2, 2 * P], F32, tag=bank_set, name="flipped")
                 for u in range(2):
                     for m in range(2):
                         nc.tensor.transpose(
                             flipped[:, u, P * m : P * (m + 1)],
-                            sorted_words[s, mp][:, m, g, u, :],
+                            words[:, m, 2 * P * g + u : 2 * P * (g + 1) : 2]
+                            if in_place
+                            else sorted_words[s, mp][:, m, g, u, :],
                             ident_f32[:],
                         )
                 flipped_banks[s, mp, g] = flipped
 
-        def quantise_pair(s, mp):
-            grouped_flat = {}
-            for g, copy in enumerate((nc.vector.tensor_copy, nc.scalar.copy)):
+        grouped_flat = {}
+
+        def regroup_pair(s, mp, copies):
+            for g, copy in enumerate(copies):
                 grouped = acts.tile(
                     [P, 2 * P, PACK], BF16, name="grouped", tag="grouped", bufs=4, align_bytes=256
                 )
-                grouped_flat[g] = grouped[:].rearrange("p b t -> p (b t)")
+                grouped_flat[s, mp, g] = grouped[:].rearrange("p b t -> p (b t)")
                 copy(
-                    out=grouped_flat[g].bitcast(F32).rearrange("p (b u) -> p b u", u=2),
+                    out=grouped_flat[s, mp, g].bitcast(F32).rearrange("p (b u) -> p b u", u=2),
                     in_=flipped_banks[s, mp, g][:].rearrange("p u b -> p b u"),
                 )
+
+        def quantise_pair(s, mp):
             for g in range(GROUPS):
                 k = GROUPS * s + g
                 z_codes[k, mp] = acts.tile(
@@ -233,7 +239,7 @@ def tile_forcedgpulstmcell_kernel(
                 nc.vector.quantize_mx(
                     out=z_codes[k, mp][:].bitcast(FP8X4),
                     scales=z_scales[k, mp][:],
-                    in_=grouped_flat[g],
+                    in_=grouped_flat[s, mp, g],
                 )
 
         def open_bank(m, first, width):
@@ -253,18 +259,19 @@ def tile_forcedgpulstmcell_kernel(
                 stop=(k == PASSES - 1),
             )
 
-        sort_words(0, 0)
-        spread_biases("bank", (GATE_I, GATE_G))
-        copy_biases((GATE_I, GATE_G))
-        transpose_pair(0, 0, "bank")
-        sort_words(0, 1)
+        spread_biases("bank", (GATE_I, GATE_G,))
+        copy_biases((GATE_I, GATE_G,))
+        transpose_pair(0, 0, "bank", in_place=True)
+        regroup_pair(0, 0, (nc.vector.tensor_copy, nc.scalar.copy))
         quantise_pair(0, 0)
-        transpose_pair(0, 1, "bank")
+        transpose_pair(0, 1, "bank", in_place=True)
+        regroup_pair(0, 1, (nc.vector.tensor_copy, nc.scalar.copy))
         sort_words(1, 0)
         quantise_pair(0, 1)
-        spread_biases("bank", (GATE_F, GATE_O))
-        copy_biases((GATE_F, GATE_O))
+        spread_biases("bank", (GATE_F, GATE_O,))
         transpose_pair(1, 0, "bank")
+        regroup_pair(1, 0, (nc.vector.tensor_copy, nc.scalar.copy))
+        copy_biases((GATE_F, GATE_O,))
         quantise_pair(1, 0)
         first_sums = []
         for m in tiles:
@@ -275,6 +282,7 @@ def tile_forcedgpulstmcell_kernel(
                 run_pass(first_sums[m], first_q, first_j, m, 0, N_TILE, k)
         sort_words(1, 1)
         transpose_pair(1, 1, "bank")
+        regroup_pair(1, 1, (nc.vector.tensor_copy, nc.scalar.copy))
         quantise_pair(1, 1)
         for m in tiles:
             for k in range(GROUPS, PASSES):
@@ -311,9 +319,9 @@ def tile_forcedgpulstmcell_kernel(
             tanh_c[j, m] = work.tile([P, N_TILE], F32, tag="tanh_c", name="tanh_c", bufs=8)
             nc.scalar.activation(out=tanh_c[j, m][:], in_=cell[j, m][:], func=TANH)
 
-        def finish_hidden(j, m, first=0, width=N_TILE):
+        def finish_hidden(j, m, first=0, width=N_TILE, engine=nc.vector):
             h_new = work.tile([P, width], F32, tag="h_new", bufs=8, align_bytes=256)
-            nc.vector.tensor_tensor(
+            engine.tensor_tensor(
                 out=h_new[:],
                 in0=gate[GATE_O, j, m, first][:],
                 in1=tanh_c[j, m][:, first : first + width],
@@ -388,8 +396,8 @@ def tile_forcedgpulstmcell_kernel(
         form_cell(1, 3)
         form_tanh(1, 3)
         finish_hidden(1, 0)
+        finish_hidden(1, 1, engine=nc.gpsimd)
         use_bank(GATE_O, 1, 2)
-        finish_hidden(1, 1)
         use_bank(GATE_O, 1, 3, 0, HALF)
         use_bank(GATE_O, 1, 3, HALF, HALF)
         finish_hidden(1, 2)

from contextlib import ExitStack

import concourse.mybir as mybir
from concourse.masks import make_identity

F32 = mybir.dt.float32
BF16 = mybir.dt.bfloat16
I32 = mybir.dt.int32
U32 = mybir.dt.uint32
U8 = mybir.dt.uint8
FP8X4 = mybir.dt.float8_e4m3fn_x4
SIGMOID = mybir.ActivationFunctionType.Sigmoid
TANH = mybir.ActivationFunctionType.Tanh
ADD = mybir.AluOpType.add
MULT = mybir.AluOpType.mult

P = 128
PACK = 4
K_PASS = P * PACK
BATCH, FEATURES, HIDDEN = 512, 1024, 1024
SOURCES = 2
GROUPS = FEATURES // K_PASS
PASSES = SOURCES * GROUPS
M_TILES = BATCH // P
M_PAIRS = M_TILES // 2
N_TILE = 512
N_HALVES = HIDDEN // N_TILE
GATES = 4
SORT_AHEAD = 1
HALF = N_TILE // 2
PLANE_ROWS = 4

FLOPS = 2 * BATCH * (SOURCES * FEATURES) * (GATES * HIDDEN)


def tile_forcedgpulstmcell_kernel(
    tc,
    x, h, c,
    weight_ii_words, weight_ii_scales, weight_if_words, weight_if_scales,
    weight_ig_words, weight_ig_scales, weight_io_words, weight_io_scales,
    weight_hi_words, weight_hi_scales, weight_hf_words, weight_hf_scales,
    weight_hg_words, weight_hg_scales, weight_ho_words, weight_ho_scales,
    bias_i, bias_f, bias_g, bias_o,
    out_0, out_1,
):
    nc = tc.nc
    gate_inputs = (
        ((weight_ii_words, weight_hi_words), (weight_ii_scales, weight_hi_scales), bias_i),
        ((weight_ig_words, weight_hg_words), (weight_ig_scales, weight_hg_scales), bias_g),
        ((weight_if_words, weight_hf_words), (weight_if_scales, weight_hf_scales), bias_f),
        ((weight_io_words, weight_ho_words), (weight_io_scales, weight_ho_scales), bias_o),
    )
    GATE_I, GATE_G, GATE_F, GATE_O = 0, 1, 2, 3
    tiles = range(M_TILES)

    with ExitStack() as ctx:
        const = ctx.enter_context(tc.tile_pool(name="const", bufs=1))
        acts = ctx.enter_context(tc.tile_pool(name="acts", bufs=1))
        weights = ctx.enter_context(tc.tile_pool(name="weights", bufs=1))
        work = ctx.enter_context(tc.tile_pool(name="work", bufs=M_TILES))
        psum = ctx.enter_context(tc.psum_pool(name="psum", bufs=2 * M_TILES))
        ctx.enter_context(tc.manual_schedule())

        bias_rows = const.tile([P, N_TILE], BF16, align_bytes=256)
        nc.vector.memset(bias_rows[:], 0.0)
        w_planes = {}
        for q in range(GATES):
            for s in range(SOURCES):
                w_planes[q, s] = weights.tile(
                    [P, HIDDEN], U8, name="w_planes_%d_%d" % (q, s), align_bytes=256
                )
                nc.vector.memset(w_planes[q, s][:].bitcast(I32), 0)
        raw = {}
        w_words = {}
        c_half = {}

        def load_bias_rows():
            for q in (GATE_I, GATE_G, GATE_F, GATE_O):
                nc.sync.dma_start(
                    out=bias_rows[N_HALVES * q : N_HALVES * (q + 1), :],
                    in_=gate_inputs[q][2].rearrange("(j n) -> j n", j=N_HALVES),
                )

        def load_pair(s, mp):
            by_pair = (x, h)[s].rearrange("(mp m p) k -> mp p m k", m=2, p=P)
            raw[s, mp] = acts.tile([P, 2, FEATURES], BF16, name="raw_%d_%d" % (s, mp), align_bytes=256)
            nc.sync.dma_start(out=raw[s, mp][:], in_=by_pair[mp])

        def load_source(s):
            for mp in range(M_PAIRS):
                load_pair(s, mp)

        def load_scales(q, s):
            for quadrant in range(4):
                first = 32 * quadrant
                nc.sync.dma_start(
                    out=w_planes[q, s][first : first + GROUPS * PLANE_ROWS, :].bitcast(I32),
                    in_=gate_inputs[q][1][s][
                        :, PLANE_ROWS * quadrant : PLANE_ROWS * (quadrant + 1), :
                    ].bitcast(I32),
                )

        def load_words(q, s, j, halves=1):
            words = weights.tile(
                [P, GROUPS, halves * N_TILE], U32, name="w_words_%d_%d_%d" % (q, s, j), align_bytes=256
            )
            by_bytes = gate_inputs[q][0][s].rearrange("g p n t -> p g (n t)")
            nc.sync.dma_start(
                out=words[:].bitcast(I32),
                in_=by_bytes[:, :, PACK * N_TILE * j : PACK * N_TILE * (j + halves)].bitcast(I32),
            )
            for half in range(j, j + halves):
                w_words[q, s, half] = (words, N_TILE * (half - j))

        def load_c(j):
            c_half[j] = acts.tile([P, M_TILES, N_TILE], BF16, name="c_half_%d" % j, align_bytes=256)
            nc.sync.dma_start(
                out=c_half[j][:],
                in_=c.rearrange("(m p) n -> p m n", p=P)[:, :, N_TILE * j : N_TILE * (j + 1)],
            )

        bias_all = const.tile([P, GATES, N_HALVES, N_TILE], BF16, align_bytes=256)

        first_q, first_j = GATE_I, 0
        load_bias_rows()
        load_pair(0, 0)
        load_pair(0, 1)
        load_pair(1, 0)
        load_scales(GATE_I, 0)
        load_words(GATE_I, 0, 0)
        load_pair(1, 1)
        load_scales(GATE_I, 1)
        load_words(GATE_I, 1, 0)
        load_scales(GATE_G, 0)
        load_words(GATE_G, 0, 0)
        load_words(GATE_G, 1, 0)
        load_scales(GATE_G, 1)
        load_scales(GATE_F, 0)
        load_words(GATE_F, 0, 0)
        load_words(GATE_F, 1, 0)
        load_scales(GATE_F, 1)
        load_c(0)
        load_words(GATE_I, 0, 1)
        load_words(GATE_I, 1, 1)
        load_words(GATE_G, 0, 1)
        load_words(GATE_G, 1, 1)
        load_words(GATE_F, 0, 1)
        load_words(GATE_F, 1, 1)
        load_c(1)
        load_scales(GATE_O, 0)
        load_words(GATE_O, 0, 0)
        load_words(GATE_O, 1, 0)
        load_scales(GATE_O, 1)
        load_words(GATE_O, 0, 1)
        load_words(GATE_O, 1, 1)

        warm = const.tile([P, 1], F32)
        nc.vector.memset(warm[:], 0.0)
        nc.scalar.activation(out=warm[:], in_=warm[:], func=SIGMOID)

        ident_bf16 = const.tile([P, P], BF16)
        ident_f32 = const.tile([P, P], F32)
        make_identity(nc, ident_bf16[:])
        make_identity(nc, ident_f32[:])

        spreads = {}

        def spread_biases(bank_set, spread_gates):
            for q in spread_gates:
                spread = psum.tile([P, N_HALVES, N_TILE], BF16, tag=bank_set, name="spread")
                for j in range(N_HALVES):
                    r = N_HALVES * q + j
                    nc.tensor.matmul(
                        out=spread[:, j, :],
                        lhsT=ident_bf16[:, r : r + 1].to_broadcast([P, P]),
                        rhs=bias_rows[:],
                        start=True,
                        stop=True,
                    )
                spreads[q] = spread

        def copy_biases(spread_gates):
            for q in spread_gates:
                nc.scalar.copy(out=bias_all[:, q, :, :], in_=spreads[q][:])

        z_codes = {}
        z_scales = {}

        sorted_words = {}
        flipped_banks = {}

        def sort_words(s, mp):
            words = raw[s, mp][:].bitcast(F32)
            sorted_words[s, mp] = acts.tile(
                [P, 2, GROUPS, 2, P], F32, name="sorted_words", tag="sorted_words", bufs=SORT_AHEAD + 1
            )
            nc.vector.tensor_copy(
                out=sorted_words[s, mp][:].rearrange("p m g u w -> p (m g) u w"),
                in_=words.rearrange("p m (g w u) -> p (m g) u w", g=GROUPS, u=2),
            )

        def transpose_pair(s, mp, bank_set, in_place=False):
            words = raw[s, mp][:].bitcast(F32)
            for g in range(GROUPS):
                flipped = psum.tile([P, 2, 2 * P], F32, tag=bank_set, name="flipped")
                for u in range(2):
                    for m in range(2):
                        nc.tensor.transpose(
                            flipped[:, u, P * m : P * (m + 1)],
                            words[:, m, 2 * P * g + u : 2 * P * (g + 1) : 2]
                            if in_place
                            else sorted_words[s, mp][:, m, g, u, :],
                            ident_f32[:],
                        )
                flipped_banks[s, mp, g] = flipped

        grouped_flat = {}

        def regroup_pair(s, mp, copies):
            for g, copy in enumerate(copies):
                grouped = acts.tile(
                    [P, 2 * P, PACK], BF16, name="grouped", tag="grouped", bufs=4, align_bytes=256
                )
                grouped_flat[s, mp, g] = grouped[:].rearrange("p b t -> p (b t)")
                copy(
                    out=grouped_flat[s, mp, g].bitcast(F32).rearrange("p (b u) -> p b u", u=2),
                    in_=flipped_banks[s, mp, g][:].rearrange("p u b -> p b u"),
                )

        def quantise_pair(s, mp):
            for g in range(GROUPS):
                k = GROUPS * s + g
                z_codes[k, mp] = acts.tile(
                    [P, 2 * P], U32, name="z_codes_%d_%d" % (k, mp), align_bytes=256
                )
                z_scales[k, mp] = acts.tile(
                    [P, 2 * P], U8, name="z_scales_%d_%d" % (k, mp), align_bytes=256
                )
                nc.vector.quantize_mx(
                    out=z_codes[k, mp][:].bitcast(FP8X4),
                    scales=z_scales[k, mp][:],
                    in_=grouped_flat[s, mp, g],
                )

        def open_bank(m, first, width):
            return psum.tile([P, width], F32, tag="bank", name="sums_%d_%d" % (m, first))

        def run_pass(sums, q, j, m, first, width, k):
            rows = slice(P * (m % 2), P * (m % 2 + 1))
            columns = slice(N_TILE * j + first, N_TILE * j + first + width)
            words, begin = w_words[q, k // GROUPS, j]
            nc.tensor.matmul_mx(
                out=sums[:],
                lhsT=z_codes[k, m // 2][:, rows].bitcast(FP8X4),
                lhsT_scale=z_scales[k, m // 2][:, rows],
                rhs=words[:, k % GROUPS, begin + first : begin + first + width].bitcast(FP8X4),
                rhs_scale=w_planes[q, k // GROUPS][PLANE_ROWS * (k % GROUPS) : P, columns],
                start=(k == 0),
                stop=(k == PASSES - 1),
            )

        spread_biases("bank", (GATE_I, GATE_G,))
        copy_biases((GATE_I, GATE_G,))
        transpose_pair(0, 0, "bank", in_place=True)
        regroup_pair(0, 0, (nc.vector.tensor_copy, nc.scalar.copy))
        quantise_pair(0, 0)
        transpose_pair(0, 1, "bank", in_place=True)
        regroup_pair(0, 1, (nc.vector.tensor_copy, nc.scalar.copy))
        sort_words(1, 0)
        quantise_pair(0, 1)
        spread_biases("bank", (GATE_F, GATE_O,))
        transpose_pair(1, 0, "bank")
        regroup_pair(1, 0, (nc.vector.tensor_copy, nc.scalar.copy))
        copy_biases((GATE_F, GATE_O,))
        quantise_pair(1, 0)
        first_sums = []
        for m in tiles:
            sums = open_bank(m, 0, N_TILE)
            first_sums.append(sums)
        for k in range(GROUPS):
            for m in tiles:
                run_pass(first_sums[m], first_q, first_j, m, 0, N_TILE, k)
        sort_words(1, 1)
        transpose_pair(1, 1, "bank")
        regroup_pair(1, 1, (nc.vector.tensor_copy, nc.scalar.copy))
        quantise_pair(1, 1)
        for m in tiles:
            for k in range(GROUPS, PASSES):
                run_pass(first_sums[m], first_q, first_j, m, 0, N_TILE, k)

        gate = {}
        new_part = {}
        kept_part = {}
        cell = {}
        tanh_c = {}

        def form_new_part(j, m):
            new_part[j, m] = work.tile([P, N_TILE], F32, tag="new_part", name="new_part")
            nc.vector.tensor_tensor(
                out=new_part[j, m][:], in0=gate[GATE_I, j, m, 0][:], in1=gate[GATE_G, j, m, 0][:], op=MULT
            )

        def form_kept_part(j, m):
            kept_part[j, m] = work.tile([P, N_TILE], F32, tag="kept_part", name="kept_part")
            nc.vector.tensor_tensor(
                out=kept_part[j, m][:], in0=gate[GATE_F, j, m, 0][:], in1=c_half[j][:, m, :], op=MULT
            )

        def form_cell(j, m):
            cell[j, m] = work.tile([P, N_TILE], F32, tag="c_new", name="c_new", bufs=8, align_bytes=256)
            nc.vector.tensor_tensor(
                out=cell[j, m][:], in0=kept_part[j, m][:], in1=new_part[j, m][:], op=ADD
            )
            nc.sync.dma_start(
                out=out_1[P * m : P * (m + 1), N_TILE * j : N_TILE * (j + 1)], in_=cell[j, m][:]
            )

        def form_tanh(j, m):
            tanh_c[j, m] = work.tile([P, N_TILE], F32, tag="tanh_c", name="tanh_c", bufs=8)
            nc.scalar.activation(out=tanh_c[j, m][:], in_=cell[j, m][:], func=TANH)

        def finish_hidden(j, m, first=0, width=N_TILE, engine=nc.vector):
            h_new = work.tile([P, width], F32, tag="h_new", bufs=8, align_bytes=256)
            engine.tensor_tensor(
                out=h_new[:],
                in0=gate[GATE_O, j, m, first][:],
                in1=tanh_c[j, m][:, first : first + width],
                op=MULT,
            )
            nc.sync.dma_start(
                out=out_0[P * m : P * (m + 1), N_TILE * j + first : N_TILE * j + first + width],
                in_=h_new[:],
            )

        def finish_hidden_beside(m):
            h_new = work.tile(
                [P, N_TILE], F32, tag="gate_%d" % GATE_F, name="gate_%d" % GATE_F, align_bytes=256
            )
            nc.gpsimd.tensor_tensor(
                out=h_new[:], in0=gate[GATE_O, 0, m, 0][:], in1=tanh_c[0, m][:], op=MULT
            )
            nc.sync.dma_start(out=out_0[P * m : P * (m + 1), 0:N_TILE], in_=h_new[:])

        gate_func = {GATE_I: SIGMOID, GATE_G: TANH, GATE_F: SIGMOID, GATE_O: SIGMOID}
        def use_bank(q, j, m, first=0, width=N_TILE):
            if (q, j) == (first_q, first_j):
                sums = first_sums[m]
            else:
                sums = open_bank(m, first, width)
                for k in range(PASSES):
                    run_pass(sums, q, j, m, first, width, k)
            value = work.tile([P, width], F32, tag="gate_%d" % q, name="gate_%d" % q, align_bytes=256)
            nc.vector.tensor_tensor(
                out=value[:], in0=sums[:], in1=bias_all[:, q, j, first : first + width], op=ADD
            )
            nc.scalar.activation(out=value[:], in_=value[:], func=gate_func[q])
            gate[q, j, m, first] = value

        for m in tiles:
            use_bank(GATE_I, 0, m)
        for m in tiles:
            use_bank(GATE_G, 0, m)
            if m >= 1:
                form_new_part(0, m - 1)
        for m in tiles:
            use_bank(GATE_F, 0, m)
            if m == 0:
                form_new_part(0, 3)
            else:
                form_kept_part(0, m - 1)
        for m in tiles:
            use_bank(GATE_I, 1, m)
            if m == 0:
                form_kept_part(0, 3)
            form_cell(0, m)
            if m > 0:
                form_tanh(0, m - 1)
        for m in tiles:
            use_bank(GATE_G, 1, m)
            if m == 0:
                form_tanh(0, 3)
            else:
                form_new_part(1, m - 1)
        for m in tiles:
            use_bank(GATE_F, 1, m)
            use_bank(GATE_O, 0, m)
            if m == 0:
                form_new_part(1, 3)
            else:
                form_cell(1, m - 1)
                form_tanh(1, m - 1)
            form_kept_part(1, m)
            finish_hidden_beside(m)
        use_bank(GATE_O, 1, 0)
        use_bank(GATE_O, 1, 1)
        form_cell(1, 3)
        form_tanh(1, 3)
        finish_hidden(1, 0)
        finish_hidden(1, 1, engine=nc.gpsimd)
        use_bank(GATE_O, 1, 2)
        use_bank(GATE_O, 1, 3, 0, HALF)
        use_bank(GATE_O, 1, 3, HALF, HALF)
        finish_hidden(1, 2)
        finish_hidden(1, 3, 0, HALF)
        finish_hidden(1, 3, HALF, HALF)
